import numpy as np
import ml_dtypes


def mxq(x, axis, fmt="e4m3"):
    dtype, down = {"e4m3": (ml_dtypes.float8_e4m3fn, 7), "e5m2": (ml_dtypes.float8_e5m2, 14)}[fmt]
    v = np.moveaxis(np.asarray(x, np.float32).astype(ml_dtypes.bfloat16).astype(np.float64), axis, -1)
    blocks = v.reshape(v.shape[:-1] + (-1, 32))
    amax = np.abs(blocks).max(-1, keepdims=True)
    byte = np.maximum(np.where(amax > 0, np.frexp(amax)[1] - 1 + 127, 0) - down, 1)
    scale = np.exp2(byte - 127.0)
    codes = (blocks / scale).astype(np.float32).astype(dtype).astype(np.float64)
    return np.moveaxis((codes * scale).reshape(v.shape), -1, axis)


WIDE = False


def mx_kscale(k):
    if not WIDE:
        return np.ones(k)
    levels = np.array([18, -18])
    if k % 512:
        return np.exp2(np.random.permutation(np.resize(levels, k // 32))).repeat(32)
    a = np.empty((k // 512, 16))
    for p in range(k // 512):
        a[p, :8] = np.random.permutation(np.resize(levels, 8))
        for g in range(8):
            far = levels[np.abs(levels - a[p, g]) >= 10]
            a[p, g + 8] = far[np.random.randint(len(far))]
    return np.exp2(a.ravel()).repeat(32)


BF16 = ml_dtypes.bfloat16


def bf(x):
    return np.asarray(x, np.float32).astype(BF16)


def f64(x):
    return np.asarray(x).astype(np.float64)


G, S, M, H, E, C = 2, 512, 512, 1024, 4, 256


def setup_inputs():
    s = mx_kscale(E * C).reshape(E, C)
    u = mx_kscale(H)
    v = mx_kscale(M)
    dm0 = bf(np.random.standard_normal((G, S, E, C)) * 0.1)
    x0 = bf(np.random.standard_normal((G, S, M)))
    wi0 = bf(np.random.standard_normal((E, M, H)) * 10.0 / np.sqrt(S * M))
    g = bf(np.random.standard_normal((E, G, C, H)) * np.exp2(np.random.randint(-6, 1, (E, G, C, 1))) * 4.0 / s[:, None, :, None] * u)
    d = f64(dm0).reshape(G, S, E * C).transpose(0, 2, 1) @ f64(x0)
    d = d.reshape(G, E, C, M).transpose(1, 0, 2, 3).reshape(E, G * C, M)
    pre = (d @ f64(wi0)).reshape(E, G, C, H)
    return {"dispatch_mask": bf(f64(dm0) * s[None, None, :, :]),
            "x": bf(f64(x0) / v),
            "wi": bf(f64(wi0) * v[None, :, None] / u),
            "pre": np.asarray(pre, np.float32),
            "grad_out": g}


def reference(dispatch_mask, x, wi, pre, grad_out):
    dz2 = (f64(grad_out) * (f64(pre) > 0.0)).reshape(E, G * C, H)
    dh = mxq(dz2, 2, "e5m2") @ mxq(f64(wi), 2, "e4m3").transpose(0, 2, 1)
    dz1 = dh.reshape(E, G, C, M).transpose(1, 0, 2, 3).reshape(G, E * C, M)
    ddm = mxq(f64(x), 2, "e4m3") @ mxq(dz1, 2, "e5m2").transpose(0, 2, 1)
    dm = f64(dispatch_mask).reshape(G, S, E * C)
    dx = mxq(dm, 2, "e4m3") @ mxq(dz1, 1, "e5m2")
    return ddm.reshape(G, S, E, C), dx

@@ -1,0 +1,350 @@
+from contextlib import ExitStack
+
+import concourse.mybir as mybir
+from concourse.masks import make_identity
+
+G, S, M, H, E, C = 2, 512, 512, 1024, 4, 256
+FLOPS = 2 * E * G * C * H * M + 2 * 2 * G * S * M * E * C
+
+F32 = mybir.dt.float32
+BF16 = mybir.dt.bfloat16
+U32 = mybir.dt.uint32
+U8 = mybir.dt.uint8
+E4M3 = mybir.dt.float8_e4m3fn_x4
+E5M2 = mybir.dt.float8_e5m2_x4
+ALU = mybir.AluOpType
+
+P = 128
+MANUAL = True
+V_OUT = (1, 3, 5, 7)
+
+
+def tile_flaxpositionwisemoelayer_pa_v_kernel(tc, dispatch_mask, x, wi, pre, grad_out, out_0, out_1):
+    nc = tc.nc
+    mask_v = dispatch_mask.rearrange("g (p t) e c -> g p t (e c)", t=4)
+    x_v = x.rearrange("g (p t) m -> g p t m", t=4)
+    wi_v = wi.rearrange("e (p t) h -> e p t h", t=4)
+    pre_v = pre.rearrange("e g c h -> e (g c) h").rearrange("e (p j) h -> e p j h", j=4)
+    go_v = grad_out.rearrange("e g c h -> e (g c) h").rearrange("e (p j) h -> e p j h", j=4)
+    out0_v = out_0.rearrange("g (p t) e c -> g p t (e c)", t=4)
+    out1_v = out_1.rearrange("g (p t) m -> g p t m", t=4)
+
+    with ExitStack() as ctx:
+        const = ctx.enter_context(tc.tile_pool(name="const", bufs=1))
+        ring = ctx.enter_context(tc.tile_pool(name="ring", bufs=1))
+        keep = ctx.enter_context(tc.tile_pool(name="keep", bufs=1))
+        psum_t = ctx.enter_context(tc.psum_pool(name="psum_t", bufs=4))
+        psum_a = ctx.enter_context(tc.psum_pool(name="psum_a", bufs=4))
+
+        ident = const.tile([P, P], F32, name="ident")
+        make_identity(nc, ident[:])
+
+        x_codes = keep.tile([P, G, S], U32, align_bytes=64, name="x_codes")
+        x_scales = keep.tile([P, G, S], U8, align_bytes=64, name="x_scales")
+        m_codes = keep.tile([P, G, 2, S], U32, align_bytes=64, name="m_codes")
+        m_scales = keep.tile([P, G, 2, S], U8, align_bytes=64, name="m_scales")
+        a_codes = keep.tile([P, 2, G, 512], U32, align_bytes=64, name="a_codes")
+        a_scales = keep.tile([P, 2, G, 512], U8, align_bytes=64, name="a_scales")
+        k_codes = keep.tile([P, 2, G, 512], U32, align_bytes=64, name="k_codes")
+        k_scales = keep.tile([P, 2, G, 512], U8, align_bytes=64, name="k_scales")
+
+        st = {}
+
+        def load_rows(key, src, n):
+            t = ring.tile([P, n, 1024], BF16, tag="rows%d" % n, bufs=6 if n == 2 else 2, align_bytes=64, name="rows")
+            nc.sync.dma_start(out=t[:], in_=src)
+            for i in range(n):
+                st[key + (i,)] = t[:, i, :]
+
+        def load_w(e, h):
+            t = ring.tile([P, 2, 1024], BF16, tag="rows", bufs=10, align_bytes=64, name="w_rows")
+            nc.sync.dma_start(out=t[:], in_=wi_v[e, :, 2 * h : 2 * h + 2, :])
+            st["w", e, 2 * h], st["w", e, 2 * h + 1] = t[:, 0, :], t[:, 1, :]
+
+        def load_m(g, h):
+            t = ring.tile([P, 2, 1024], BF16, tag="rows", bufs=10, align_bytes=64, name="m_rows")
+            nc.sync.dma_start(out=t[:], in_=mask_v[g, :, 2 * h : 2 * h + 2, :])
+            st["m", g, 2 * h], st["m", g, 2 * h + 1] = t[:, 0, :], t[:, 1, :]
+
+        def load_go(e, h):
+            t = ring.tile([P, 2, 1024], BF16, tag="rows", bufs=10, align_bytes=64, name="go_rows")
+            nc.sync.dma_start(out=t[:], in_=go_v[e, :, 2 * h : 2 * h + 2, :])
+            st["go", e, 2 * h], st["go", e, 2 * h + 1] = t[:, 0, :], t[:, 1, :]
+
+        def load_pre(e, h):
+            t = ring.tile([P, 2, 1024], F32, tag="pre", bufs=4, align_bytes=64, name="pre_rows")
+            nc.sync.dma_start(out=t[:], in_=pre_v[e, :, 2 * h : 2 * h + 2, :])
+            st["pre", e, 2 * h], st["pre", e, 2 * h + 1] = t[:, 0, :], t[:, 1, :]
+
+        def load_x(g):
+            t = ring.tile([P, 4, 512], BF16, tag="x", bufs=2, align_bytes=64, name="x_rows")
+            nc.sync.dma_start(out=t[:], in_=x_v[g])
+            st["x", g] = t
+
+        def stt(e, j):
+            t = ring.tile([P, 1024], BF16, tag="dz2", bufs=4, align_bytes=64, name="dz2")
+            nc.vector.scalar_tensor_tensor(
+                out=t[:],
+                in0=st["pre", e, j],
+                scalar=0.0,
+                in1=st["go", e, j],
+                op0=ALU.is_gt,
+                op1=ALU.mult,
+            )
+            st["dz2", e, j] = t
+
+        def grouped(key):
+            if key not in st:
+                st[key] = ring.tile([P, 2, 512, 4], BF16, tag="grp", bufs=3, align_bytes=64, name="grp")
+            return st[key]
+
+        def t_rows(key, words, is_sorted):
+            bank = psum_t.tile([P, 2, 2, P], F32, tag="t", name="bank_t")
+            for a in range(2):
+                for u in range(2):
+                    if is_sorted:
+                        src = words[:, 256 * a + 128 * u : 256 * a + 128 * (u + 1)]
+                    else:
+                        src = words[:, 256 * a + u : 256 * (a + 1) : 2]
+                    nc.tensor.transpose(bank[:, a, u, :], src, ident[:])
+            st[("bank",) + key] = bank
+
+        def copy(engine, out, in_):
+            if engine == "s":
+                nc.scalar.copy(out=out, in_=in_)
+            else:
+                nc.vector.tensor_copy(out=out, in_=in_)
+
+        def c_rows(engine, key, gkey, j):
+            grp = grouped(gkey)
+            bank = st[("bank",) + key]
+            dst = grp[:].rearrange("p a r k -> p a (r k)").bitcast(F32)[:, :, 256 * j : 256 * (j + 1)]
+            copy(engine, dst.rearrange("p a (r u) -> p a r u", u=2), bank[:].rearrange("p a u r -> p a r u"))
+
+        def t_w(e, t):
+            t_rows(("w", e, t), st["w", e, t].bitcast(F32), False)
+
+        def c_w(e, t, eng="s"):
+            c_rows(eng, ("w", e, t), ("gw", e), t)
+
+        def t_d(e, j):
+            t_rows(("d", e, j), st["dz2", e, j][:].bitcast(F32), False)
+
+        def c_d(e, j, eng="s"):
+            c_rows(eng, ("d", e, j), ("gd", e), j)
+
+        def t_m(g, t):
+            t_rows(("m", g, t), st["m", g, t].bitcast(F32), False)
+
+        def c_m(g, t, eng="s"):
+            c_rows(eng, ("m", g, t), ("gm", g), t)
+
+        def q_rows(gkey, dt, out_codes, out_scales):
+            for a in range(2):
+                nc.vector.quantize_mx(
+                    out=out_codes[a].bitcast(dt), scales=out_scales[a],
+                    in_=st[gkey][:, a, :, :].rearrange("p r k -> p (r k)"))
+
+        def q_w(e):
+            codes = ring.tile([P, 2, 512], U32, tag="wc", bufs=2, align_bytes=64, name="w_codes")
+            scales = ring.tile([P, 2, 512], U8, tag="ws", bufs=2, align_bytes=64, name="w_scales")
+            q_rows(("gw", e), E4M3, [codes[:, a, :] for a in range(2)], [scales[:, a, :] for a in range(2)])
+            st["wq", e] = (codes, scales)
+
+        def q_d(e):
+            codes = ring.tile([P, 2, 512], U32, tag="dc", bufs=2, align_bytes=64, name="d_codes")
+            scales = ring.tile([P, 2, 512], U8, tag="ds", bufs=2, align_bytes=64, name="d_scales")
+            q_rows(("gd", e), E5M2, [codes[:, a, :] for a in range(2)], [scales[:, a, :] for a in range(2)])
+            st["dq", e] = (codes, scales)
+
+        def q_m(g):
+            q_rows(("gm", g), E4M3, [m_codes[:, g, a, :] for a in range(2)], [m_scales[:, g, a, :] for a in range(2)])
+
+        def t_x(g, h):
+            bank = psum_t.tile([P, 2, 2, P], F32, tag="t", name="bank_t")
+            for i in range(2):
+                words = st["x", g][:, 2 * h + i, :].bitcast(F32)
+                for u in range(2):
+                    nc.tensor.transpose(bank[:, i, u, :], words[:, u::2], ident[:])
+            st["bank", "x", g, h] = bank
+
+        def c_x(g, h, eng="s"):
+            if ("gx", g) not in st:
+                st["gx", g] = ring.tile([P, 512, 4], BF16, tag="gx", bufs=2, align_bytes=64, name="gx")
+            dst = st["gx", g][:].rearrange("p r k -> p (r k)").bitcast(F32)[:, 512 * h : 512 * (h + 1)]
+            copy(eng, dst.rearrange("p (i r u) -> p i r u", i=2, u=2),
+                 st["bank", "x", g, h][:].rearrange("p i u r -> p i r u"))
+
+        def q_x(g):
+            nc.vector.quantize_mx(out=x_codes[:, g, :].bitcast(E4M3), scales=x_scales[:, g, :],
+                                  in_=st["gx", g][:].rearrange("p r k -> p (r k)"))
+
+        def mm1(e, t):
+            wc, ws = st["wq", e]
+            dc, ds = st["dq", e]
+            acc = psum_a.tile([P, 512], F32, tag="a", name="acc")
+            for a in range(2):
+                nc.tensor.matmul_mx(
+                    out=acc[:], lhsT=wc[:, a, 128 * t : 128 * (t + 1)].bitcast(E4M3),
+                    lhsT_scale=ws[:, a, 128 * t : 128 * (t + 1)],
+                    rhs=dc[:, a, :].bitcast(E5M2), rhs_scale=ds[:, a, :],
+                    start=(a == 0), stop=(a == 1))
+            st["acc", e, t] = acc
+
+        def c_dh(e, t, eng="s"):
+            pair, i = divmod(e, 2)
+            if ("dz1", pair) not in st:
+                st["dz1", pair] = ring.tile([P, 4, G, 512], BF16, tag="dz1", bufs=2, align_bytes=64, name="dz1")
+            dst = st["dz1", pair][:, t, :, 256 * i : 256 * (i + 1)].rearrange("p g (q j) -> p g q j", j=4)
+            copy(eng, dst, st["acc", e, t][:].rearrange("p (j g q) -> p g q j", j=4, g=2))
+
+        def i_a(e, g, eng="v"):
+            pair, i = divmod(e, 2)
+            t = ring.tile([P, 256, 4], BF16, tag="ga", bufs=4, align_bytes=64, name="ga")
+            copy(eng, t[:], st["dz1", pair][:, :, g, 256 * i : 256 * (i + 1)].rearrange("p t s -> p s t"))
+            st["ga", e, g] = t
+
+        def q_a(e, g):
+            pair, i = divmod(e, 2)
+            nc.vector.quantize_mx(
+                out=a_codes[:, pair, g, 256 * i : 256 * (i + 1)].bitcast(E5M2),
+                scales=a_scales[:, pair, g, 256 * i : 256 * (i + 1)],
+                in_=st["ga", e, g][:].rearrange("p s t -> p (s t)"))
+
+        def t_s(pair, g, h):
+            bank = psum_t.tile([P, 2, 2, P], F32, tag="t", name="bank_t")
+            for i in range(2):
+                words = st["dz1", pair][:, 2 * h + i, g, :].bitcast(F32)
+                for u in range(2):
+                    nc.tensor.transpose(bank[:, i, u, :], words[:, u::2], ident[:])
+            st["bank", "s", pair, g, h] = bank
+
+        def c_s(pair, g, h, eng="s"):
+            if ("gs", pair, g) not in st:
+                st["gs", pair, g] = ring.tile([P, 512, 4], BF16, tag="gs", bufs=2, align_bytes=64, name="gs")
+            dst = st["gs", pair, g][:].rearrange("p m k -> p (m k)").bitcast(F32)[:, 512 * h : 512 * (h + 1)]
+            copy(eng, dst.rearrange("p (i m u) -> p i m u", i=2, u=2),
+                 st["bank", "s", pair, g, h][:].rearrange("p i u m -> p i m u"))
+
+        def q_s(pair, g):
+            nc.vector.quantize_mx(
+                out=k_codes[:, pair, g, :].bitcast(E5M2), scales=k_scales[:, pair, g, :],
+                in_=st["gs", pair, g][:].rearrange("p m k -> p (m k)"))
+
+        def mm_o0(pair, g, t):
+            acc = psum_a.tile([P, 512], F32, tag="a", name="acc")
+            nc.tensor.matmul_mx(
+                out=acc[:], lhsT=x_codes[:, g, 128 * t : 128 * (t + 1)].bitcast(E4M3),
+                lhsT_scale=x_scales[:, g, 128 * t : 128 * (t + 1)],
+                rhs=a_codes[:, pair, g, :].bitcast(E5M2), rhs_scale=a_scales[:, pair, g, :],
+                start=True, stop=True)
+            st["o0", pair, g, t] = acc
+
+        def c_o0(pair, g, t, eng):
+            if t % 2 == 0:
+                st["r0"] = ring.tile([P, 2, 512], F32, tag="res", bufs=7, align_bytes=64, name="res")
+            copy(eng, st["r0"][:, t % 2, :], st["o0", pair, g, t][:])
+            if t % 2 == 1:
+                nc.sync.dma_start(out=out0_v[g, :, t - 1 : t + 1, 512 * pair : 512 * (pair + 1)], in_=st["r0"][:])
+
+        def mm_o1(g, t):
+            acc = psum_a.tile([P, 512], F32, tag="a", name="acc")
+            for pair in range(2):
+                nc.tensor.matmul_mx(
+                    out=acc[:], lhsT=m_codes[:, g, pair, 128 * t : 128 * (t + 1)].bitcast(E4M3),
+                    lhsT_scale=m_scales[:, g, pair, 128 * t : 128 * (t + 1)],
+                    rhs=k_codes[:, pair, g, :].bitcast(E5M2), rhs_scale=k_scales[:, pair, g, :],
+                    start=(pair == 0), stop=(pair == 1))
+            st["o1", g, t] = acc
+
+        def c_o1(g, t, eng):
+            if t % 2 == 0:
+                st["r1"] = ring.tile([P, 2, 512], F32, tag="res", bufs=7, align_bytes=64, name="res")
+            copy(eng, st["r1"][:, t % 2, :].rearrange("p (m t) -> p m t", t=4),
+                 st["o1", g, t][:].rearrange("p (t m) -> p m t", t=4))
+            if t % 2 == 1:
+                nc.sync.dma_start(out=out1_v[g, :, t - 1 : t + 1, :], in_=st["r1"][:])
+
+        def run():
+            loads = [lambda: load_pre(0, 0), lambda: load_go(0, 0), lambda: load_x(0), lambda: load_w(0, 0),
+                     lambda: load_pre(0, 1), lambda: load_go(0, 1), lambda: load_w(0, 1), lambda: load_x(1)]
+            for f in loads:
+                f()
+
+            def load_half(hh):
+                if hh < 8:
+                    load_pre(hh // 2, hh % 2)
+                    load_go(hh // 2, hh % 2)
+                    load_w(hh // 2, hh % 2)
+
+            load_half(2)
+            load_half(3)
+            for k in range(0, 26):
+                e, i = divmod(k, 4)
+                if k < 16:
+                    stt(e, i)
+                if k < 4:
+                    t_x(k // 2, k % 2)
+                    c_x(k // 2, k % 2)
+                    if k % 2 == 1:
+                        q_x(k // 2)
+                if k < 16:
+                    t_w(e, i)
+                    c_w(e, i)
+                    if i % 2 == 1:
+                        load_half(k // 2 + 4)
+                if k in (9, 11):
+                    for h in range(2):
+                        load_m((k - 9) // 2, h)
+                if 1 <= k <= 16:
+                    ed, jd = divmod(k - 1, 4)
+                    t_d(ed, jd)
+                    c_d(ed, jd)
+                if k >= 17 and k < 25:
+                    t_m((k - 17) // 4, (k - 17) % 4)
+                    c_m((k - 17) // 4, (k - 17) % 4)
+                    if (k - 17) % 4 == 3:
+                        q_m((k - 17) // 4)
+                if i == 0 and 1 <= e <= 4:
+                    q_w(e - 1)
+                if i == 1 and 1 <= e <= 4:
+                    q_d(e - 1)
+                if 6 <= k < 22:
+                    em, tm = divmod(k - 6, 4)
+                    mm1(em, tm)
+                    c_dh(em, tm)
+                ei, gi = divmod(k - 10, 4)
+                if 0 <= ei < 4 and gi < 2:
+                    i_a(ei, gi)
+                ei, gi = divmod(k - 11, 4)
+                if 0 <= ei < 4 and gi < 2:
+                    q_a(ei, gi)
+                if 14 <= k < 18:
+                    t_s(0, (k - 14) // 2, k % 2)
+                    c_s(0, (k - 14) // 2, k % 2)
+                if k == 16 or k == 18:
+                    q_s(0, (k - 16) // 2)
+                if 17 <= k < 21:
+                    for t in (2 * (k - 17), 2 * (k - 17) + 1):
+                        mm_o0(0, t // 4, t % 4)
+                        c_o0(0, t // 4, t % 4, "sv"[t % 2])
+            for g in range(2):
+                for t in range(4):
+                    mm_o0(1, g, t)
+                    c_o0(1, g, t, "sv"[t % 2])
+                if g == 0:
+                    for gg in range(2):
+                        for h in range(2):
+                            t_s(1, gg, h)
+                            c_s(1, gg, h, "sv"[h])
+                        q_s(1, gg)
+            for g in range(2):
+                for t in range(4):
+                    mm_o1(g, t)
+                    c_o1(g, t, "sv"[t % 2])
+
+        if MANUAL:
+            with tc.manual_schedule():
+                run()
+        else:
+            run()

@@ -15,8 +15,37 @@ E5M2 = mybir.dt.float8_e5m2_x4
 ALU = mybir.AluOpType
 
 P = 128
-MANUAL = True
-V_OUT = (1, 3, 5, 7)
+NGRP = 3
+NWC = 2
+NDC = 1
+NDZ = 2
+NGA = 2
+NGS = 2
+NRES = 7
+NPRE = 4
+NROWS = 10
+PLAN = (
+    "lw.0.0 lp1.0.0 lp1.0.1 lw.0.1 lpre.0.1 lgo.0.1 lw.1.0 lpre.1.0 lgo.1.0 lw.1.1 lpre.1.1 lgo.1.1 lw.2.0 lx.0 "
+    "lx.1 tw.0.0 tw.0.1 cw.0.0.s cw.0.1.v stt.0.0 td.0.0 stt.0.1 lpre.2.0 lgo.2.0 lw.2.1 cd.0.0.s tw.0.2 td.0.1 "
+    "cw.0.2.s tw.0.3 cd.0.1.v cw.0.3.s qw.0.0 qw.0.1 stt.0.2 tw.1.0 stt.0.3 lpre.2.1 lgo.2.1 lw.3.0 tw.1.1 cw.1.0.s "
+    "td.0.2 cw.1.1.s td.0.3 cd.0.2.v cd.0.3.s qd.0.0 stt.1.0 tw.1.2 stt.1.1 lpre.3.0 lgo.3.0 lw.3.1 tw.1.3 cw.1.2.s "
+    "td.1.0 cw.1.3.s qd.0.1 td.1.1 cd.1.0.s qw.1.0 m1.0.0 cd.1.1.s qw.1.1 m1.0.1 cdh.0.0.s stt.1.2 m1.0.2 cdh.0.1.s "
+    "m1.0.3 cdh.0.2.s stt.1.3 lpre.3.1 lgo.3.1 lm.0.0 lm.0.1 td.1.2 cdh.0.3.s tw.2.0 cd.1.2.s ia.0.0 td.1.3 cw.2.0.s "
+    "tx.0.0 ia.0.1 cd.1.3.s tx.0.1 qa.0.0 cx.0.0.s qa.0.1 tw.2.1 lm.1.0 qd.1.0 cx.0.1.s tx.1.0 qd.1.1 tx.1.1 "
+    "cw.2.1.s qx.0 cx.1.0.s m1.1.0 cx.1.1.v m1.1.1 cdh.1.0.s stt.2.0 m1.1.2 cdh.1.1.s m1.1.3 cdh.1.2.s stt.2.1 lm.1.1 "
+    "ts.0.0.0 cdh.1.3.s ts.0.1.0 qx.1 cs.0.0.0.s ts.0.0.1 ia.1.0 cs.0.1.0.s ts.0.1.1 cs.0.0.1.s ia.1.1 td.2.0 cs.0.1.1.s td.2.1 "
+    "qa.1.0 qa.1.1 cd.2.0.s tw.2.2 stt.2.2 cd.2.1.s o0.0.0.0 tw.2.3 cw.2.2.s stt.2.3 td.2.2 co0.0.0.0.s o0.0.0.1 cw.2.3.s "
+    "cd.2.2.v tw.3.0 co0.0.0.1.s qw.2.0 td.2.3 cw.3.0.s qw.2.1 tw.3.1 cd.2.3.s qs.0.0 o0.0.0.2 cw.3.1.s o0.0.0.3 stt.3.0 "
+    "o0.0.1.0 o0.0.1.1 co0.0.0.2.s tw.3.2 co0.0.0.3.s stt.3.1 td.3.0 co0.0.1.0.s tw.3.3 cw.3.2.s cd.3.0.v o0.0.1.2 cw.3.3.s qd.2.0 "
+    "td.3.1 co0.0.1.1.s qd.2.1 o0.0.1.3 cd.3.1.s stt.3.2 m1.2.0 co0.0.1.2.s m1.2.1 co0.0.1.3.s stt.3.3 m1.2.2 cdh.2.0.s td.3.2 "
+    "cdh.2.1.s qw.3.0 td.3.3 cdh.2.2.s cd.3.2.v m1.2.3 cd.3.3.s qw.3.1 tm.0.0 cdh.2.3.s qd.3.0 tm.0.1 qd.3.1 cm.0.0.s "
+    "tm.0.2 cm.0.1.s ia.2.0 m1.3.0 cm.0.2.s ia.2.1 m1.3.1 cdh.3.0.s qa.2.0 m1.3.2 qa.2.1 cdh.3.1.s m1.3.3 qs.0.1 "
+    "cdh.3.2.s tm.0.3 cdh.3.3.v tm.1.0 cm.0.3.s ia.3.0 tm.1.1 cm.1.0.s qm.0.0 tm.1.2 cm.1.1.s tm.1.3 qa.3.0 qm.0.1 "
+    "cm.1.2.s o0.1.0.0 o0.1.0.1 ia.3.1 cm.1.3.s o0.1.0.2 o0.1.0.3 co0.1.0.0.s co0.1.0.1.v ts.1.0.0 co0.1.0.2.s qa.3.1 ts.1.0.1 qm.1.0 "
+    "co0.1.0.3.s o0.1.1.0 qm.1.1 cs.1.0.0.s o0.1.1.1 o0.1.1.2 co0.1.1.0.v cs.1.0.1.s o0.1.1.3 ts.1.1.0 co0.1.1.1.v co0.1.1.2.s ts.1.1.1 qs.1.0 "
+    "co0.1.1.3.s cs.1.1.0.v cs.1.1.1.s o1.0.0 o1.0.1 qs.1.1 co1.0.0.s o1.0.2 co1.0.1.v o1.0.3 co1.0.2.s o1.1.0 co1.0.3.v o1.1.1 "
+    "co1.1.0.s o1.1.2 co1.1.1.v o1.1.3 co1.1.2.s co1.1.3.v "
+)
 
 
 def tile_flaxpositionwisemoelayer_pa_v_kernel(tc, dispatch_mask, x, wi, pre, grad_out, out_0, out_1):
@@ -50,31 +79,35 @@ def tile_flaxpositionwisemoelayer_pa_v_kernel(tc, dispatch_mask, x, wi, pre, gra
 
         st = {}
 
-        def load_rows(key, src, n):
-            t = ring.tile([P, n, 1024], BF16, tag="rows%d" % n, bufs=6 if n == 2 else 2, align_bytes=64, name="rows")
-            nc.sync.dma_start(out=t[:], in_=src)
-            for i in range(n):
-                st[key + (i,)] = t[:, i, :]
-
         def load_w(e, h):
-            t = ring.tile([P, 2, 1024], BF16, tag="rows", bufs=10, align_bytes=64, name="w_rows")
+            t = ring.tile([P, 2, 1024], BF16, tag="rows", bufs=NROWS, align_bytes=64, name="w_rows")
             nc.sync.dma_start(out=t[:], in_=wi_v[e, :, 2 * h : 2 * h + 2, :])
             st["w", e, 2 * h], st["w", e, 2 * h + 1] = t[:, 0, :], t[:, 1, :]
 
         def load_m(g, h):
-            t = ring.tile([P, 2, 1024], BF16, tag="rows", bufs=10, align_bytes=64, name="m_rows")
+            t = ring.tile([P, 2, 1024], BF16, tag="rows", bufs=NROWS, align_bytes=64, name="m_rows")
             nc.sync.dma_start(out=t[:], in_=mask_v[g, :, 2 * h : 2 * h + 2, :])
             st["m", g, 2 * h], st["m", g, 2 * h + 1] = t[:, 0, :], t[:, 1, :]
 
         def load_go(e, h):
-            t = ring.tile([P, 2, 1024], BF16, tag="rows", bufs=10, align_bytes=64, name="go_rows")
+            t = ring.tile([P, 2, 1024], BF16, tag="rows", bufs=NROWS, align_bytes=64, name="go_rows")
             nc.sync.dma_start(out=t[:], in_=go_v[e, :, 2 * h : 2 * h + 2, :])
             st["go", e, 2 * h], st["go", e, 2 * h + 1] = t[:, 0, :], t[:, 1, :]
 
         def load_pre(e, h):
-            t = ring.tile([P, 2, 1024], F32, tag="pre", bufs=4, align_bytes=64, name="pre_rows")
+            t = ring.tile([P, 2, 1024], F32, tag="pre", bufs=NPRE, align_bytes=64, name="pre_rows")
             nc.sync.dma_start(out=t[:], in_=pre_v[e, :, 2 * h : 2 * h + 2, :])
             st["pre", e, 2 * h], st["pre", e, 2 * h + 1] = t[:, 0, :], t[:, 1, :]
+
+        def load_pre1(e, j):
+            h = j // 2
+            if j % 2 == 0:
+                st["pt", e, h] = ring.tile([P, 2, 1024], F32, tag="pre", bufs=NPRE, align_bytes=64, name="pre_rows")
+                st["gt", e, h] = ring.tile([P, 2, 1024], BF16, tag="rows", bufs=NROWS, align_bytes=64, name="go_rows")
+            for key, tile_key, src in (("pre", "pt", pre_v), ("go", "gt", go_v)):
+                t = st[tile_key, e, h]
+                nc.sync.dma_start(out=t[:, j % 2, :], in_=src[e, :, j, :])
+                st[key, e, j] = t[:, j % 2, :]
 
         def load_x(g):
             t = ring.tile([P, 4, 512], BF16, tag="x", bufs=2, align_bytes=64, name="x_rows")
@@ -82,7 +115,7 @@ def tile_flaxpositionwisemoelayer_pa_v_kernel(tc, dispatch_mask, x, wi, pre, gra
             st["x", g] = t
 
         def stt(e, j):
-            t = ring.tile([P, 1024], BF16, tag="dz2", bufs=4, align_bytes=64, name="dz2")
+            t = ring.tile([P, 1024], BF16, tag="dz2", bufs=NDZ, align_bytes=64, name="dz2")
             nc.vector.scalar_tensor_tensor(
                 out=t[:],
                 in0=st["pre", e, j],
@@ -95,7 +128,7 @@ def tile_flaxpositionwisemoelayer_pa_v_kernel(tc, dispatch_mask, x, wi, pre, gra
 
         def grouped(key):
             if key not in st:
-                st[key] = ring.tile([P, 2, 512, 4], BF16, tag="grp", bufs=3, align_bytes=64, name="grp")
+                st[key] = ring.tile([P, 2, 512, 4], BF16, tag="grp", bufs=NGRP, align_bytes=64, name="grp")
             return st[key]
 
         def t_rows(key, words, is_sorted):
@@ -139,26 +172,26 @@ def tile_flaxpositionwisemoelayer_pa_v_kernel(tc, dispatch_mask, x, wi, pre, gra
         def c_m(g, t, eng="s"):
             c_rows(eng, ("m", g, t), ("gm", g), t)
 
-        def q_rows(gkey, dt, out_codes, out_scales):
-            for a in range(2):
-                nc.vector.quantize_mx(
-                    out=out_codes[a].bitcast(dt), scales=out_scales[a],
-                    in_=st[gkey][:, a, :, :].rearrange("p r k -> p (r k)"))
+        def q_rows(gkey, a, dt, out_codes, out_scales):
+            nc.vector.quantize_mx(
+                out=out_codes.bitcast(dt), scales=out_scales, in_=st[gkey][:, a, :, :].rearrange("p r k -> p (r k)"))
 
-        def q_w(e):
-            codes = ring.tile([P, 2, 512], U32, tag="wc", bufs=2, align_bytes=64, name="w_codes")
-            scales = ring.tile([P, 2, 512], U8, tag="ws", bufs=2, align_bytes=64, name="w_scales")
-            q_rows(("gw", e), E4M3, [codes[:, a, :] for a in range(2)], [scales[:, a, :] for a in range(2)])
-            st["wq", e] = (codes, scales)
+        def q_w(e, a):
+            if ("wq", e) not in st:
+                st["wq", e] = (ring.tile([P, 2, 512], U32, tag="wc", bufs=NWC, align_bytes=64, name="w_codes"),
+                               ring.tile([P, 2, 512], U8, tag="ws", bufs=NWC, align_bytes=64, name="w_scales"))
+            codes, scales = st["wq", e]
+            q_rows(("gw", e), a, E4M3, codes[:, a, :], scales[:, a, :])
 
-        def q_d(e):
-            codes = ring.tile([P, 2, 512], U32, tag="dc", bufs=2, align_bytes=64, name="d_codes")
-            scales = ring.tile([P, 2, 512], U8, tag="ds", bufs=2, align_bytes=64, name="d_scales")
-            q_rows(("gd", e), E5M2, [codes[:, a, :] for a in range(2)], [scales[:, a, :] for a in range(2)])
-            st["dq", e] = (codes, scales)
+        def q_d(e, a):
+            if ("dq", e) not in st:
+                st["dq", e] = (ring.tile([P, 2, 512], U32, tag="dc", bufs=NDC, align_bytes=64, name="d_codes"),
+                               ring.tile([P, 2, 512], U8, tag="ds", bufs=NDC, align_bytes=64, name="d_scales"))
+            codes, scales = st["dq", e]
+            q_rows(("gd", e), a, E5M2, codes[:, a, :], scales[:, a, :])
 
-        def q_m(g):
-            q_rows(("gm", g), E4M3, [m_codes[:, g, a, :] for a in range(2)], [m_scales[:, g, a, :] for a in range(2)])
+        def q_m(g, a):
+            q_rows(("gm", g), a, E4M3, m_codes[:, g, a, :], m_scales[:, g, a, :])
 
         def t_x(g, h):
             bank = psum_t.tile([P, 2, 2, P], F32, tag="t", name="bank_t")
@@ -200,7 +233,7 @@ def tile_flaxpositionwisemoelayer_pa_v_kernel(tc, dispatch_mask, x, wi, pre, gra
 
         def i_a(e, g, eng="v"):
             pair, i = divmod(e, 2)
-            t = ring.tile([P, 256, 4], BF16, tag="ga", bufs=4, align_bytes=64, name="ga")
+            t = ring.tile([P, 256, 4], BF16, tag="ga", bufs=NGA, align_bytes=64, name="ga")
             copy(eng, t[:], st["dz1", pair][:, :, g, 256 * i : 256 * (i + 1)].rearrange("p t s -> p s t"))
             st["ga", e, g] = t
 
@@ -221,7 +254,7 @@ def tile_flaxpositionwisemoelayer_pa_v_kernel(tc, dispatch_mask, x, wi, pre, gra
 
         def c_s(pair, g, h, eng="s"):
             if ("gs", pair, g) not in st:
-                st["gs", pair, g] = ring.tile([P, 512, 4], BF16, tag="gs", bufs=2, align_bytes=64, name="gs")
+                st["gs", pair, g] = ring.tile([P, 512, 4], BF16, tag="gs", bufs=NGS, align_bytes=64, name="gs")
             dst = st["gs", pair, g][:].rearrange("p m k -> p (m k)").bitcast(F32)[:, 512 * h : 512 * (h + 1)]
             copy(eng, dst.rearrange("p (i m u) -> p i m u", i=2, u=2),
                  st["bank", "s", pair, g, h][:].rearrange("p i u m -> p i m u"))
@@ -241,11 +274,14 @@ def tile_flaxpositionwisemoelayer_pa_v_kernel(tc, dispatch_mask, x, wi, pre, gra
             st["o0", pair, g, t] = acc
 
         def c_o0(pair, g, t, eng):
-            if t % 2 == 0:
-                st["r0"] = ring.tile([P, 2, 512], F32, tag="res", bufs=7, align_bytes=64, name="res")
-            copy(eng, st["r0"][:, t % 2, :], st["o0", pair, g, t][:])
-            if t % 2 == 1:
-                nc.sync.dma_start(out=out0_v[g, :, t - 1 : t + 1, 512 * pair : 512 * (pair + 1)], in_=st["r0"][:])
+            key = ("r0", pair, g, t // 2)
+            first = key not in st
+            if first:
+                st[key] = ring.tile([P, 2, 512], F32, tag="res", bufs=NRES, align_bytes=64, name="res")
+            copy(eng, st[key][:, t % 2, :], st["o0", pair, g, t][:])
+            if not first:
+                t = t - t % 2
+                nc.sync.dma_start(out=out0_v[g, :, t : t + 2, 512 * pair : 512 * (pair + 1)], in_=st[key][:])
 
         def mm_o1(g, t):
             acc = psum_a.tile([P, 512], F32, tag="a", name="acc")
@@ -258,93 +294,20 @@ def tile_flaxpositionwisemoelayer_pa_v_kernel(tc, dispatch_mask, x, wi, pre, gra
             st["o1", g, t] = acc
 
         def c_o1(g, t, eng):
-            if t % 2 == 0:
-                st["r1"] = ring.tile([P, 2, 512], F32, tag="res", bufs=7, align_bytes=64, name="res")
-            copy(eng, st["r1"][:, t % 2, :].rearrange("p (m t) -> p m t", t=4),
+            key = ("r1", g, t // 2)
+            first = key not in st
+            if first:
+                st[key] = ring.tile([P, 2, 512], F32, tag="res", bufs=NRES, align_bytes=64, name="res")
+            copy(eng, st[key][:, t % 2, :].rearrange("p (m t) -> p m t", t=4),
                  st["o1", g, t][:].rearrange("p (t m) -> p m t", t=4))
-            if t % 2 == 1:
-                nc.sync.dma_start(out=out1_v[g, :, t - 1 : t + 1, :], in_=st["r1"][:])
+            if not first:
+                t = t - t % 2
+                nc.sync.dma_start(out=out1_v[g, :, t : t + 2, :], in_=st[key][:])
 
-        def run():
-            loads = [lambda: load_pre(0, 0), lambda: load_go(0, 0), lambda: load_x(0), lambda: load_w(0, 0),
-                     lambda: load_pre(0, 1), lambda: load_go(0, 1), lambda: load_w(0, 1), lambda: load_x(1)]
-            for f in loads:
-                f()
-
-            def load_half(hh):
-                if hh < 8:
-                    load_pre(hh // 2, hh % 2)
-                    load_go(hh // 2, hh % 2)
-                    load_w(hh // 2, hh % 2)
-
-            load_half(2)
-            load_half(3)
-            for k in range(0, 26):
-                e, i = divmod(k, 4)
-                if k < 16:
-                    stt(e, i)
-                if k < 4:
-                    t_x(k // 2, k % 2)
-                    c_x(k // 2, k % 2)
-                    if k % 2 == 1:
-                        q_x(k // 2)
-                if k < 16:
-                    t_w(e, i)
-                    c_w(e, i)
-                    if i % 2 == 1:
-                        load_half(k // 2 + 4)
-                if k in (9, 11):
-                    for h in range(2):
-                        load_m((k - 9) // 2, h)
-                if 1 <= k <= 16:
-                    ed, jd = divmod(k - 1, 4)
-                    t_d(ed, jd)
-                    c_d(ed, jd)
-                if k >= 17 and k < 25:
-                    t_m((k - 17) // 4, (k - 17) % 4)
-                    c_m((k - 17) // 4, (k - 17) % 4)
-                    if (k - 17) % 4 == 3:
-                        q_m((k - 17) // 4)
-                if i == 0 and 1 <= e <= 4:
-                    q_w(e - 1)
-                if i == 1 and 1 <= e <= 4:
-                    q_d(e - 1)
-                if 6 <= k < 22:
-                    em, tm = divmod(k - 6, 4)
-                    mm1(em, tm)
-                    c_dh(em, tm)
-                ei, gi = divmod(k - 10, 4)
-                if 0 <= ei < 4 and gi < 2:
-                    i_a(ei, gi)
-                ei, gi = divmod(k - 11, 4)
-                if 0 <= ei < 4 and gi < 2:
-                    q_a(ei, gi)
-                if 14 <= k < 18:
-                    t_s(0, (k - 14) // 2, k % 2)
-                    c_s(0, (k - 14) // 2, k % 2)
-                if k == 16 or k == 18:
-                    q_s(0, (k - 16) // 2)
-                if 17 <= k < 21:
-                    for t in (2 * (k - 17), 2 * (k - 17) + 1):
-                        mm_o0(0, t // 4, t % 4)
-                        c_o0(0, t // 4, t % 4, "sv"[t % 2])
-            for g in range(2):
-                for t in range(4):
-                    mm_o0(1, g, t)
-                    c_o0(1, g, t, "sv"[t % 2])
-                if g == 0:
-                    for gg in range(2):
-                        for h in range(2):
-                            t_s(1, gg, h)
-                            c_s(1, gg, h, "sv"[h])
-                        q_s(1, gg)
-            for g in range(2):
-                for t in range(4):
-                    mm_o1(g, t)
-                    c_o1(g, t, "sv"[t % 2])
-
-        if MANUAL:
-            with tc.manual_schedule():
-                run()
-        else:
-            run()
+        table = dict(stt=stt, tw=t_w, cw=c_w, td=t_d, cd=c_d, tx=t_x, cx=c_x, qx=q_x, tm=t_m, cm=c_m, qw=q_w, qd=q_d, qm=q_m,
+                     m1=mm1, cdh=c_dh, ia=i_a, qa=q_a, ts=t_s, cs=c_s, qs=q_s, o0=mm_o0, co0=c_o0, o1=mm_o1, co1=c_o1,
+                     lpre=load_pre, lgo=load_go, lw=load_w, lx=load_x, lm=load_m, lp1=load_pre1)
+        with tc.manual_schedule():
+            for token in PLAN.split():
+                part = token.split(".")
+                table[part[0]](*[int(a) if a not in ("s", "v") else a for a in part[1:]])

@@ -13,134 +13,86 @@ U8 = mybir.dt.uint8
 E4M3 = mybir.dt.float8_e4m3fn_x4
 E5M2 = mybir.dt.float8_e5m2_x4
 ALU = mybir.AluOpType
-
 P = 128
 NGRP = 3
 NWC = 2
-NDC = 1
+NDC = 2
 NDZ = 2
-NGA = 2
+NGA = 1
 NGS = 2
-NRES = 7
+NRES = 6
 NPRE = 4
-NROWS = 10
+NGO = 2
+NWM = 3
 PLAN = (
-    "lw.0.0 lp1.0.0 lp1.0.1 lw.0.1 lpre.0.1 lgo.0.1 lw.1.0 lpre.1.0 lgo.1.0 lw.1.1 lpre.1.1 lgo.1.1 lw.2.0 lx.0 "
-    "lx.1 tw.0.0 tw.0.1 cw.0.0.s cw.0.1.v stt.0.0 td.0.0 stt.0.1 lpre.2.0 lgo.2.0 lw.2.1 cd.0.0.s tw.0.2 td.0.1 "
-    "cw.0.2.s tw.0.3 cd.0.1.v cw.0.3.s qw.0.0 qw.0.1 stt.0.2 tw.1.0 stt.0.3 lpre.2.1 lgo.2.1 lw.3.0 tw.1.1 cw.1.0.s "
-    "td.0.2 cw.1.1.s td.0.3 cd.0.2.v cd.0.3.s qd.0.0 stt.1.0 tw.1.2 stt.1.1 lpre.3.0 lgo.3.0 lw.3.1 tw.1.3 cw.1.2.s "
-    "td.1.0 cw.1.3.s qd.0.1 td.1.1 cd.1.0.s qw.1.0 m1.0.0 cd.1.1.s qw.1.1 m1.0.1 cdh.0.0.s stt.1.2 m1.0.2 cdh.0.1.s "
-    "m1.0.3 cdh.0.2.s stt.1.3 lpre.3.1 lgo.3.1 lm.0.0 lm.0.1 td.1.2 cdh.0.3.s tw.2.0 cd.1.2.s ia.0.0 td.1.3 cw.2.0.s "
-    "tx.0.0 ia.0.1 cd.1.3.s tx.0.1 qa.0.0 cx.0.0.s qa.0.1 tw.2.1 lm.1.0 qd.1.0 cx.0.1.s tx.1.0 qd.1.1 tx.1.1 "
-    "cw.2.1.s qx.0 cx.1.0.s m1.1.0 cx.1.1.v m1.1.1 cdh.1.0.s stt.2.0 m1.1.2 cdh.1.1.s m1.1.3 cdh.1.2.s stt.2.1 lm.1.1 "
-    "ts.0.0.0 cdh.1.3.s ts.0.1.0 qx.1 cs.0.0.0.s ts.0.0.1 ia.1.0 cs.0.1.0.s ts.0.1.1 cs.0.0.1.s ia.1.1 td.2.0 cs.0.1.1.s td.2.1 "
-    "qa.1.0 qa.1.1 cd.2.0.s tw.2.2 stt.2.2 cd.2.1.s o0.0.0.0 tw.2.3 cw.2.2.s stt.2.3 td.2.2 co0.0.0.0.s o0.0.0.1 cw.2.3.s "
-    "cd.2.2.v tw.3.0 co0.0.0.1.s qw.2.0 td.2.3 cw.3.0.s qw.2.1 tw.3.1 cd.2.3.s qs.0.0 o0.0.0.2 cw.3.1.s o0.0.0.3 stt.3.0 "
-    "o0.0.1.0 o0.0.1.1 co0.0.0.2.s tw.3.2 co0.0.0.3.s stt.3.1 td.3.0 co0.0.1.0.s tw.3.3 cw.3.2.s cd.3.0.v o0.0.1.2 cw.3.3.s qd.2.0 "
-    "td.3.1 co0.0.1.1.s qd.2.1 o0.0.1.3 cd.3.1.s stt.3.2 m1.2.0 co0.0.1.2.s m1.2.1 co0.0.1.3.s stt.3.3 m1.2.2 cdh.2.0.s td.3.2 "
-    "cdh.2.1.s qw.3.0 td.3.3 cdh.2.2.s cd.3.2.v m1.2.3 cd.3.3.s qw.3.1 tm.0.0 cdh.2.3.s qd.3.0 tm.0.1 qd.3.1 cm.0.0.s "
-    "tm.0.2 cm.0.1.s ia.2.0 m1.3.0 cm.0.2.s ia.2.1 m1.3.1 cdh.3.0.s qa.2.0 m1.3.2 qa.2.1 cdh.3.1.s m1.3.3 qs.0.1 "
-    "cdh.3.2.s tm.0.3 cdh.3.3.v tm.1.0 cm.0.3.s ia.3.0 tm.1.1 cm.1.0.s qm.0.0 tm.1.2 cm.1.1.s tm.1.3 qa.3.0 qm.0.1 "
-    "cm.1.2.s o0.1.0.0 o0.1.0.1 ia.3.1 cm.1.3.s o0.1.0.2 o0.1.0.3 co0.1.0.0.s co0.1.0.1.v ts.1.0.0 co0.1.0.2.s qa.3.1 ts.1.0.1 qm.1.0 "
-    "co0.1.0.3.s o0.1.1.0 qm.1.1 cs.1.0.0.s o0.1.1.1 o0.1.1.2 co0.1.1.0.v cs.1.0.1.s o0.1.1.3 ts.1.1.0 co0.1.1.1.v co0.1.1.2.s ts.1.1.1 qs.1.0 "
-    "co0.1.1.3.s cs.1.1.0.v cs.1.1.1.s o1.0.0 o1.0.1 qs.1.1 co1.0.0.s o1.0.2 co1.0.1.v o1.0.3 co1.0.2.s o1.1.0 co1.0.3.v o1.1.1 "
-    "co1.1.0.s o1.1.2 co1.1.1.v o1.1.3 co1.1.2.s co1.1.3.v "
+    "lw.0.0.2 lw.0.2.2 lpre.0.0.1 lgo.0.0.1 lpre.0.1.1 lgo.0.1.1 lpre.0.2.2 lgo.0.2.2 lw.1.0.2 lpre.1.0.2 lgo.1.0.2 lw.1.2.2 lpre.1.2.2 lgo.1.2.2 "
+    "lx.0 lx.1 lw.2.0.2 w.0.0.s w.0.1.v stt.0 stt.1 lpre.2.0.2 w.0.2.s w.0.3.v stt.2 stt.3 lgo.2.0.2 lw.2.2.2 "
+    "lpre.2.2.2 lgo.2.2.2 lw.3.0.2 lw.3.2.2 qw.0 d.0.0.s d.0.1.s d.0.2.v d.0.3.v w.1.0.s w.1.1.s qd.0 m1.0.0.s stt.4 "
+    "stt.5 lpre.3.0.2 stt.6 stt.7 lgo.3.0.2 lpre.3.2.2 lgo.3.2.2 m1.0.1.v d.1.0.s d.1.1.s w.1.2.s w.1.3.s lm.0.0.2 lm.0.2.2 "
+    "qw.1 m1.0.2.v d.1.2.s d.1.3.s m1.0.3.s x.0.0.s x.0.1.s qd.1 ia.0 x.1.0.s x.1.1.s stt.8 stt.9 m1.1.0.s "
+    "qx m1.1.1.s m1.1.2.s m1.1.3.s ia.1 w.2.0.s w.2.1.s s.0.0.0.s s.0.0.1.s w.2.2.s w.2.3.s lm.1.0.2 lm.1.2.2 s.0.1.0.s "
+    "s.0.1.1.s stt.10 stt.11 d.2.0.v d.2.1.s d.2.2.s d.2.3.s qa.0.0 qw.2 qd.2 o0.0.0.0.s o0.0.0.1.s w.3.0.s w.3.1.s "
+    "o0.0.0.2.s o0.0.0.3.s qs.0.0 stt.12 stt.13 stt.14 stt.15 m1.2.0.s qa.0.1 m1.2.1.s m1.2.2.s m1.2.3.v w.3.2.s w.3.3.s "
+    "d.3.0.s d.3.1.s qw.3 d.3.2.s d.3.3.s qd.3 ia.2 m.0.0.s m.0.1.s o0.0.1.0.s o0.0.1.1.s m.0.2.s m.0.3.v m1.3.0.s "
+    "m1.3.1.v m1.3.2.s m1.3.3.s qm.0 ia.3 m.1.0.s m.1.1.s o0.0.1.2.s o0.0.1.3.s m.1.2.s m.1.3.s qa.1.0 qa.1.1 qs.0.1 "
+    "o0.1.0.0.v o0.1.0.1.s s.1.0.0.s s.1.0.1.v o0.1.0.2.s o0.1.0.3.v o0.1.1.0.s o0.1.1.1.s qs.1.0 qm.1 s.1.1.0.v s.1.1.1.v o0.1.1.2.s o0.1.1.3.s "
+    "o1a.0.0 o1a.0.1 qs.1.1 o1.0.0.s o1.0.1.s o1a.0.2 o1a.0.3 o1.0.2.v o1.0.3.s o1a.1.0 o1a.1.1 o1.1.0.s o1.1.1.v o1a.1.2 "
+    "o1a.1.3 o1.1.2.v o1.1.3.s "
 )
 
 
 def tile_flaxpositionwisemoelayer_pa_v_kernel(tc, dispatch_mask, x, wi, pre, grad_out, out_0, out_1):
     nc = tc.nc
-    mask_v = dispatch_mask.rearrange("g (p t) e c -> g p t (e c)", t=4)
-    x_v = x.rearrange("g (p t) m -> g p t m", t=4)
-    wi_v = wi.rearrange("e (p t) h -> e p t h", t=4)
-    pre_v = pre.rearrange("e g c h -> e (g c) h").rearrange("e (p j) h -> e p j h", j=4)
-    go_v = grad_out.rearrange("e g c h -> e (g c) h").rearrange("e (p j) h -> e p j h", j=4)
-    out0_v = out_0.rearrange("g (p t) e c -> g p t (e c)", t=4)
-    out1_v = out_1.rearrange("g (p t) m -> g p t m", t=4)
+    mask_rows = dispatch_mask.rearrange("g (p t) e c -> g p t (e c)", t=4)
+    x_rows = x.rearrange("g (p t) m -> g p t m", t=4)
+    wi_rows = wi.rearrange("e (p t) h -> e p t h", t=4)
+    pre_rows = pre.rearrange("e g c h -> e (g c) h").rearrange("e (p j) h -> e p j h", j=4)
+    grad_rows = grad_out.rearrange("e g c h -> e (g c) h").rearrange("e (p j) h -> e p j h", j=4)
+    out0_rows = out_0.rearrange("g (p t) e c -> g p t (e c)", t=4)
+    out1_rows = out_1.rearrange("g (p t) m -> g p t m", t=4)
 
     with ExitStack() as ctx:
-        const = ctx.enter_context(tc.tile_pool(name="const", bufs=1))
-        ring = ctx.enter_context(tc.tile_pool(name="ring", bufs=1))
         keep = ctx.enter_context(tc.tile_pool(name="keep", bufs=1))
-        psum_t = ctx.enter_context(tc.psum_pool(name="psum_t", bufs=4))
-        psum_a = ctx.enter_context(tc.psum_pool(name="psum_a", bufs=4))
+        ring = ctx.enter_context(tc.tile_pool(name="ring", bufs=1))
+        psum = ctx.enter_context(tc.psum_pool(name="psum", bufs=4))
 
-        ident = const.tile([P, P], F32, name="ident")
+        ident = keep.tile([P, P], F32, name="ident")
         make_identity(nc, ident[:])
-
-        x_codes = keep.tile([P, G, S], U32, align_bytes=64, name="x_codes")
-        x_scales = keep.tile([P, G, S], U8, align_bytes=64, name="x_scales")
-        m_codes = keep.tile([P, G, 2, S], U32, align_bytes=64, name="m_codes")
-        m_scales = keep.tile([P, G, 2, S], U8, align_bytes=64, name="m_scales")
-        a_codes = keep.tile([P, 2, G, 512], U32, align_bytes=64, name="a_codes")
-        a_scales = keep.tile([P, 2, G, 512], U8, align_bytes=64, name="a_scales")
-        k_codes = keep.tile([P, 2, G, 512], U32, align_bytes=64, name="k_codes")
-        k_scales = keep.tile([P, 2, G, 512], U8, align_bytes=64, name="k_scales")
-
+        x_codes = keep.tile([P, G * S], U32, align_bytes=64, name="x_codes")
+        x_scales = keep.tile([P, G * S], U8, align_bytes=64, name="x_scales")
+        mask_codes = keep.tile([P, G, 2 * S], U32, align_bytes=64, name="mask_codes")
+        mask_scales = keep.tile([P, G, 2 * S], U8, align_bytes=64, name="mask_scales")
+        dm_codes = keep.tile([P, 2, G, 512], U32, align_bytes=64, name="dm_codes")
+        dm_scales = keep.tile([P, 2, G, 512], U8, align_bytes=64, name="dm_scales")
+        dk_codes = keep.tile([P, 2, G, 512], U32, align_bytes=64, name="dk_codes")
+        dk_scales = keep.tile([P, 2, G, 512], U8, align_bytes=64, name="dk_scales")
         st = {}
 
-        def load_w(e, h):
-            t = ring.tile([P, 2, 1024], BF16, tag="rows", bufs=NROWS, align_bytes=64, name="w_rows")
-            nc.sync.dma_start(out=t[:], in_=wi_v[e, :, 2 * h : 2 * h + 2, :])
-            st["w", e, 2 * h], st["w", e, 2 * h + 1] = t[:, 0, :], t[:, 1, :]
-
-        def load_m(g, h):
-            t = ring.tile([P, 2, 1024], BF16, tag="rows", bufs=NROWS, align_bytes=64, name="m_rows")
-            nc.sync.dma_start(out=t[:], in_=mask_v[g, :, 2 * h : 2 * h + 2, :])
-            st["m", g, 2 * h], st["m", g, 2 * h + 1] = t[:, 0, :], t[:, 1, :]
-
-        def load_go(e, h):
-            t = ring.tile([P, 2, 1024], BF16, tag="rows", bufs=NROWS, align_bytes=64, name="go_rows")
-            nc.sync.dma_start(out=t[:], in_=go_v[e, :, 2 * h : 2 * h + 2, :])
-            st["go", e, 2 * h], st["go", e, 2 * h + 1] = t[:, 0, :], t[:, 1, :]
-
-        def load_pre(e, h):
-            t = ring.tile([P, 2, 1024], F32, tag="pre", bufs=NPRE, align_bytes=64, name="pre_rows")
-            nc.sync.dma_start(out=t[:], in_=pre_v[e, :, 2 * h : 2 * h + 2, :])
-            st["pre", e, 2 * h], st["pre", e, 2 * h + 1] = t[:, 0, :], t[:, 1, :]
-
-        def load_pre1(e, j):
-            h = j // 2
-            if j % 2 == 0:
-                st["pt", e, h] = ring.tile([P, 2, 1024], F32, tag="pre", bufs=NPRE, align_bytes=64, name="pre_rows")
-                st["gt", e, h] = ring.tile([P, 2, 1024], BF16, tag="rows", bufs=NROWS, align_bytes=64, name="go_rows")
-            for key, tile_key, src in (("pre", "pt", pre_v), ("go", "gt", go_v)):
-                t = st[tile_key, e, h]
-                nc.sync.dma_start(out=t[:, j % 2, :], in_=src[e, :, j, :])
-                st[key, e, j] = t[:, j % 2, :]
-
-        def load_x(g):
-            t = ring.tile([P, 4, 512], BF16, tag="x", bufs=2, align_bytes=64, name="x_rows")
-            nc.sync.dma_start(out=t[:], in_=x_v[g])
-            st["x", g] = t
-
-        def stt(e, j):
-            t = ring.tile([P, 1024], BF16, tag="dz2", bufs=NDZ, align_bytes=64, name="dz2")
-            nc.vector.scalar_tensor_tensor(
-                out=t[:],
-                in0=st["pre", e, j],
-                scalar=0.0,
-                in1=st["go", e, j],
-                op0=ALU.is_gt,
-                op1=ALU.mult,
-            )
-            st["dz2", e, j] = t
-
-        def grouped(key):
+        def tile_of(key, shape, dtype, tag, bufs):
             if key not in st:
-                st[key] = ring.tile([P, 2, 512, 4], BF16, tag="grp", bufs=NGRP, align_bytes=64, name="grp")
+                st[key] = ring.tile(shape, dtype, tag=tag, bufs=bufs, align_bytes=64, name="t_" + tag)
             return st[key]
 
-        def t_rows(key, words, is_sorted):
-            bank = psum_t.tile([P, 2, 2, P], F32, tag="t", name="bank_t")
-            for a in range(2):
-                for u in range(2):
-                    if is_sorted:
-                        src = words[:, 256 * a + 128 * u : 256 * a + 128 * (u + 1)]
-                    else:
-                        src = words[:, 256 * a + u : 256 * (a + 1) : 2]
-                    nc.tensor.transpose(bank[:, a, u, :], src, ident[:])
-            st[("bank",) + key] = bank
+        def load(key, src, dtype, tag, bufs, j, n):
+            t = tile_of(key, [P, 4, src.shape[-1]], dtype, tag, bufs)
+            nc.sync.dma_start(out=t[:, j : j + n, :], in_=src[:, j : j + n, :])
+
+        def load_pre(e, j, n):
+            h = j // 2
+            t = tile_of(("pre", e, h), [P, 2, H], F32, "pre", NPRE)
+            nc.sync.dma_start(out=t[:, j - 2 * h : j - 2 * h + n, :], in_=pre_rows[e, :, j : j + n, :])
+
+        def load_go(e, j, n):
+            load(("go", e), grad_rows[e], BF16, "go", NGO, j, n)
+
+        def load_w(e, j, n):
+            load(("w", e), wi_rows[e], BF16, "wm", NWM, j, n)
+
+        def load_m(g, j, n):
+            load(("m", g), mask_rows[g], BF16, "wm", NWM, j, n)
+
+        def load_x(g):
+            load(("x", g), x_rows[g], BF16, "x", 2, 0, 4)
 
         def copy(engine, out, in_):
             if engine == "s":
@@ -148,166 +100,134 @@ def tile_flaxpositionwisemoelayer_pa_v_kernel(tc, dispatch_mask, x, wi, pre, gra
             else:
                 nc.vector.tensor_copy(out=out, in_=in_)
 
-        def c_rows(engine, key, gkey, j):
-            grp = grouped(gkey)
-            bank = st[("bank",) + key]
-            dst = grp[:].rearrange("p a r k -> p a (r k)").bitcast(F32)[:, :, 256 * j : 256 * (j + 1)]
-            copy(engine, dst.rearrange("p a (r u) -> p a r u", u=2), bank[:].rearrange("p a u r -> p a r u"))
+        def stt(n):
+            e, j = divmod(n, 4)
+            h, u = divmod(j, 2)
+            dz2 = tile_of(("dz2", e, h), [P, 2, 2, 512], BF16, "dz2", NDZ)
+            nc.vector.scalar_tensor_tensor(
+                out=dz2[:, u].rearrange("p j (k b) -> p j k b", b=2),
+                in0=st["pre", e, h][:].rearrange("p j (k u b) -> p u j k b", u=2, b=2)[:, u],
+                scalar=0.0,
+                in1=st["go", e][:, 2 * h : 2 * h + 2, :].rearrange("p j (k u b) -> p u j k b", u=2, b=2)[:, u],
+                op0=ALU.is_gt,
+                op1=ALU.mult,
+            )
 
-        def t_w(e, t):
-            t_rows(("w", e, t), st["w", e, t].bitcast(F32), False)
+        def new_bank():
+            bank = psum.tile([P, 2, 2, P], F32, tag="turn", bufs=4, name="bank")
+            return bank
 
-        def c_w(e, t, eng="s"):
-            c_rows(eng, ("w", e, t), ("gw", e), t)
-
-        def t_d(e, j):
-            t_rows(("d", e, j), st["dz2", e, j][:].bitcast(F32), False)
-
-        def c_d(e, j, eng="s"):
-            c_rows(eng, ("d", e, j), ("gd", e), j)
-
-        def t_m(g, t):
-            t_rows(("m", g, t), st["m", g, t].bitcast(F32), False)
-
-        def c_m(g, t, eng="s"):
-            c_rows(eng, ("m", g, t), ("gm", g), t)
-
-        def q_rows(gkey, a, dt, out_codes, out_scales):
-            nc.vector.quantize_mx(
-                out=out_codes.bitcast(dt), scales=out_scales, in_=st[gkey][:, a, :, :].rearrange("p r k -> p (r k)"))
-
-        def q_w(e, a):
-            if ("wq", e) not in st:
-                st["wq", e] = (ring.tile([P, 2, 512], U32, tag="wc", bufs=NWC, align_bytes=64, name="w_codes"),
-                               ring.tile([P, 2, 512], U8, tag="ws", bufs=NWC, align_bytes=64, name="w_scales"))
-            codes, scales = st["wq", e]
-            q_rows(("gw", e), a, E4M3, codes[:, a, :], scales[:, a, :])
-
-        def q_d(e, a):
-            if ("dq", e) not in st:
-                st["dq", e] = (ring.tile([P, 2, 512], U32, tag="dc", bufs=NDC, align_bytes=64, name="d_codes"),
-                               ring.tile([P, 2, 512], U8, tag="ds", bufs=NDC, align_bytes=64, name="d_scales"))
-            codes, scales = st["dq", e]
-            q_rows(("gd", e), a, E5M2, codes[:, a, :], scales[:, a, :])
-
-        def q_m(g, a):
-            q_rows(("gm", g), a, E4M3, m_codes[:, g, a, :], m_scales[:, g, a, :])
-
-        def t_x(g, h):
-            bank = psum_t.tile([P, 2, 2, P], F32, tag="t", name="bank_t")
+        def turn(eng, srcs, grp, block):
+            bank = psum.tile([P, 2, 2, P], F32, tag="turn", bufs=4, name="bank")
             for i in range(2):
-                words = st["x", g][:, 2 * h + i, :].bitcast(F32)
                 for u in range(2):
-                    nc.tensor.transpose(bank[:, i, u, :], words[:, u::2], ident[:])
-            st["bank", "x", g, h] = bank
+                    nc.tensor.transpose(bank[:, i, u, :], srcs(i, u), ident[:])
+            dst = grp[:].bitcast(F32)[:, 512 * block : 512 * (block + 1)]
+            copy(eng, dst.rearrange("p (i r u) -> p i r u", i=2, u=2), bank[:].rearrange("p i u r -> p i r u"))
 
-        def c_x(g, h, eng="s"):
-            if ("gx", g) not in st:
-                st["gx", g] = ring.tile([P, 512, 4], BF16, tag="gx", bufs=2, align_bytes=64, name="gx")
-            dst = st["gx", g][:].rearrange("p r k -> p (r k)").bitcast(F32)[:, 512 * h : 512 * (h + 1)]
-            copy(eng, dst.rearrange("p (i r u) -> p i r u", i=2, u=2),
-                 st["bank", "x", g, h][:].rearrange("p i u r -> p i r u"))
+        def grouped(key):
+            return tile_of(key, [P, 4096], BF16, "grp", NGRP)
 
-        def q_x(g):
-            nc.vector.quantize_mx(out=x_codes[:, g, :].bitcast(E4M3), scales=x_scales[:, g, :],
-                                  in_=st["gx", g][:].rearrange("p r k -> p (r k)"))
+        def w(e, t, eng):
+            words = st["w", e][:, t, :].bitcast(F32)
+            turn(eng, lambda a, u: words[:, 256 * a + u : 256 * (a + 1) : 2], grouped(("gw", e)), t)
 
-        def mm1(e, t):
-            wc, ws = st["wq", e]
-            dc, ds = st["dq", e]
-            acc = psum_a.tile([P, 512], F32, tag="a", name="acc")
+        def m(g, t, eng):
+            words = st["m", g][:, t, :].bitcast(F32)
+            turn(eng, lambda a, u: words[:, 256 * a + u : 256 * (a + 1) : 2], grouped(("gm", g)), t)
+
+        def d(e, j, eng):
+            h, a = divmod(j, 2)
+            dz2 = st["dz2", e, h]
+            turn(eng, lambda jj, u: dz2[:, u, jj, 256 * a : 256 * (a + 1)].bitcast(F32), grouped(("gd", e)), 2 * a + h)
+
+        def quantize(grp, dt, codes, scales):
+            nc.vector.quantize_mx(out=codes.bitcast(dt), scales=scales, in_=grp)
+
+        def qw(e):
+            codes = tile_of(("wc", e), [P, 1024], U32, "wc", NWC)
+            scales = tile_of(("ws", e), [P, 1024], U8, "ws", NWC)
+            quantize(st["gw", e][:], E4M3, codes[:], scales[:])
+
+        def qd(e):
+            codes = tile_of(("dc", e), [P, 1024], U32, "dc", NDC)
+            scales = tile_of(("ds", e), [P, 1024], U8, "ds", NDC)
+            quantize(st["gd", e][:], E5M2, codes[:], scales[:])
+
+        def qm(g):
+            quantize(st["gm", g][:], E4M3, mask_codes[:, g, :], mask_scales[:, g, :])
+
+        def x_(g, h, eng):
+            rows = st["x", g]
+            turn(eng, lambda i, u: rows[:, 2 * h + i, :].bitcast(F32)[:, u::2], tile_of(("gx",), [P, 4096], BF16, "gx", 1), 2 * g + h)
+
+        def qx():
+            quantize(st["gx",][:], E4M3, x_codes[:], x_scales[:])
+
+        def m1(e, t, eng):
+            pair, i = divmod(e, 2)
+            acc = psum.tile([P, 512], F32, tag="acc", bufs=4, name="acc")
             for a in range(2):
+                wcols = slice(256 * t + 128 * a, 256 * t + 128 * (a + 1))
+                dcols = slice(512 * a, 512 * (a + 1))
                 nc.tensor.matmul_mx(
-                    out=acc[:], lhsT=wc[:, a, 128 * t : 128 * (t + 1)].bitcast(E4M3),
-                    lhsT_scale=ws[:, a, 128 * t : 128 * (t + 1)],
-                    rhs=dc[:, a, :].bitcast(E5M2), rhs_scale=ds[:, a, :],
+                    out=acc[:], lhsT=st["wc", e][:, wcols].bitcast(E4M3), lhsT_scale=st["ws", e][:, wcols],
+                    rhs=st["dc", e][:, dcols].bitcast(E5M2), rhs_scale=st["ds", e][:, dcols],
                     start=(a == 0), stop=(a == 1))
-            st["acc", e, t] = acc
+            dz1 = tile_of(("dz1", pair), [P, 4, G, 2, 256], BF16, "dz1", 2)
+            copy(eng, dz1[:, t, :, :, 128 * i : 128 * (i + 1)].rearrange("p g u (q b) -> p g u q b", b=2),
+                 acc[:].rearrange("p (u b g q) -> p g u q b", u=2, b=2, g=2))
 
-        def c_dh(e, t, eng="s"):
+        def ia(e):
             pair, i = divmod(e, 2)
-            if ("dz1", pair) not in st:
-                st["dz1", pair] = ring.tile([P, 4, G, 512], BF16, tag="dz1", bufs=2, align_bytes=64, name="dz1")
-            dst = st["dz1", pair][:, t, :, 256 * i : 256 * (i + 1)].rearrange("p g (q j) -> p g q j", j=4)
-            copy(eng, dst, st["acc", e, t][:].rearrange("p (j g q) -> p g q j", j=4, g=2))
+            ga = tile_of(("ga", pair), [P, G, 2, 2, 128, 4], BF16, "ga", NGA)
+            nc.vector.tensor_copy(out=ga[:, :, i], in_=st["dz1", pair][:, :, :, :, 128 * i : 128 * (i + 1)].rearrange("p t g u s -> p g u s t"))
 
-        def i_a(e, g, eng="v"):
-            pair, i = divmod(e, 2)
-            t = ring.tile([P, 256, 4], BF16, tag="ga", bufs=NGA, align_bytes=64, name="ga")
-            copy(eng, t[:], st["dz1", pair][:, :, g, 256 * i : 256 * (i + 1)].rearrange("p t s -> p s t"))
-            st["ga", e, g] = t
+        def qa(pair, g):
+            quantize(st["ga", pair][:, g].rearrange("p i u s t -> p (i u s t)"), E5M2, dm_codes[:, pair, g, :], dm_scales[:, pair, g, :])
 
-        def q_a(e, g):
-            pair, i = divmod(e, 2)
-            nc.vector.quantize_mx(
-                out=a_codes[:, pair, g, 256 * i : 256 * (i + 1)].bitcast(E5M2),
-                scales=a_scales[:, pair, g, 256 * i : 256 * (i + 1)],
-                in_=st["ga", e, g][:].rearrange("p s t -> p (s t)"))
+        def s(pair, g, h, eng):
+            dz1 = st["dz1", pair]
+            turn(eng, lambda i, u: dz1[:, 2 * h + i, g, u, :].bitcast(F32), tile_of(("gs", pair, g), [P, 2048], BF16, "gs", NGS), h)
 
-        def t_s(pair, g, h):
-            bank = psum_t.tile([P, 2, 2, P], F32, tag="t", name="bank_t")
-            for i in range(2):
-                words = st["dz1", pair][:, 2 * h + i, g, :].bitcast(F32)
-                for u in range(2):
-                    nc.tensor.transpose(bank[:, i, u, :], words[:, u::2], ident[:])
-            st["bank", "s", pair, g, h] = bank
+        def qs(pair, g):
+            quantize(st["gs", pair, g][:], E5M2, dk_codes[:, pair, g, :], dk_scales[:, pair, g, :])
 
-        def c_s(pair, g, h, eng="s"):
-            if ("gs", pair, g) not in st:
-                st["gs", pair, g] = ring.tile([P, 512, 4], BF16, tag="gs", bufs=NGS, align_bytes=64, name="gs")
-            dst = st["gs", pair, g][:].rearrange("p m k -> p (m k)").bitcast(F32)[:, 512 * h : 512 * (h + 1)]
-            copy(eng, dst.rearrange("p (i m u) -> p i m u", i=2, u=2),
-                 st["bank", "s", pair, g, h][:].rearrange("p i u m -> p i m u"))
-
-        def q_s(pair, g):
-            nc.vector.quantize_mx(
-                out=k_codes[:, pair, g, :].bitcast(E5M2), scales=k_scales[:, pair, g, :],
-                in_=st["gs", pair, g][:].rearrange("p m k -> p (m k)"))
-
-        def mm_o0(pair, g, t):
-            acc = psum_a.tile([P, 512], F32, tag="a", name="acc")
+        def o0(pair, g, t, eng):
+            acc = psum.tile([P, 512], F32, tag="acc", bufs=4, name="acc")
+            cols = slice(512 * g + 128 * t, 512 * g + 128 * (t + 1))
             nc.tensor.matmul_mx(
-                out=acc[:], lhsT=x_codes[:, g, 128 * t : 128 * (t + 1)].bitcast(E4M3),
-                lhsT_scale=x_scales[:, g, 128 * t : 128 * (t + 1)],
-                rhs=a_codes[:, pair, g, :].bitcast(E5M2), rhs_scale=a_scales[:, pair, g, :],
-                start=True, stop=True)
-            st["o0", pair, g, t] = acc
+                out=acc[:], lhsT=x_codes[:, cols].bitcast(E4M3), lhsT_scale=x_scales[:, cols],
+                rhs=dm_codes[:, pair, g, :].bitcast(E5M2), rhs_scale=dm_scales[:, pair, g, :], start=True, stop=True)
+            res = tile_of(("r0", pair, g, t // 2), [P, 2, 512], F32, "res", NRES)
+            copy(eng, res[:, t % 2, :].rearrange("p (i q u b) -> p i q u b", i=2, u=2, b=2),
+                 acc[:].rearrange("p (i u q b) -> p i q u b", i=2, u=2, b=2))
+            if t % 2 == 1:
+                nc.sync.dma_start(out=out0_rows[g, :, t - 1 : t + 1, 512 * pair : 512 * (pair + 1)], in_=res[:])
 
-        def c_o0(pair, g, t, eng):
-            key = ("r0", pair, g, t // 2)
-            first = key not in st
-            if first:
-                st[key] = ring.tile([P, 2, 512], F32, tag="res", bufs=NRES, align_bytes=64, name="res")
-            copy(eng, st[key][:, t % 2, :], st["o0", pair, g, t][:])
-            if not first:
-                t = t - t % 2
-                nc.sync.dma_start(out=out0_v[g, :, t : t + 2, 512 * pair : 512 * (pair + 1)], in_=st[key][:])
+        def o1_pass(g, t, pair):
+            if pair == 0:
+                tag = "acc" if g == 0 else "turn"
+                st["o1", g, t] = psum.tile([P, 512], F32, tag=tag, bufs=4, name="acc1")
+            cols = slice(256 * t + 128 * pair, 256 * t + 128 * (pair + 1))
+            nc.tensor.matmul_mx(
+                out=st["o1", g, t][:], lhsT=mask_codes[:, g, cols].bitcast(E4M3), lhsT_scale=mask_scales[:, g, cols],
+                rhs=dk_codes[:, pair, g, :].bitcast(E5M2), rhs_scale=dk_scales[:, pair, g, :],
+                start=(pair == 0), stop=(pair == 1))
 
-        def mm_o1(g, t):
-            acc = psum_a.tile([P, 512], F32, tag="a", name="acc")
-            for pair in range(2):
-                nc.tensor.matmul_mx(
-                    out=acc[:], lhsT=m_codes[:, g, pair, 128 * t : 128 * (t + 1)].bitcast(E4M3),
-                    lhsT_scale=m_scales[:, g, pair, 128 * t : 128 * (t + 1)],
-                    rhs=k_codes[:, pair, g, :].bitcast(E5M2), rhs_scale=k_scales[:, pair, g, :],
-                    start=(pair == 0), stop=(pair == 1))
-            st["o1", g, t] = acc
+        def o1a(g, t):
+            o1_pass(g, t, 0)
 
-        def c_o1(g, t, eng):
-            key = ("r1", g, t // 2)
-            first = key not in st
-            if first:
-                st[key] = ring.tile([P, 2, 512], F32, tag="res", bufs=NRES, align_bytes=64, name="res")
-            copy(eng, st[key][:, t % 2, :].rearrange("p (m t) -> p m t", t=4),
-                 st["o1", g, t][:].rearrange("p (t m) -> p m t", t=4))
-            if not first:
-                t = t - t % 2
-                nc.sync.dma_start(out=out1_v[g, :, t : t + 2, :], in_=st[key][:])
+        def o1(g, t, eng):
+            o1_pass(g, t, 1)
+            res = tile_of(("r1", g, t // 2), [P, 2, 512], F32, "res", NRES)
+            copy(eng, res[:, t % 2, :].rearrange("p (m t) -> p m t", t=4), st["o1", g, t][:].rearrange("p (t m) -> p m t", t=4))
+            if t % 2 == 1:
+                nc.sync.dma_start(out=out1_rows[g, :, t - 1 : t + 1, :], in_=res[:])
 
-        table = dict(stt=stt, tw=t_w, cw=c_w, td=t_d, cd=c_d, tx=t_x, cx=c_x, qx=q_x, tm=t_m, cm=c_m, qw=q_w, qd=q_d, qm=q_m,
-                     m1=mm1, cdh=c_dh, ia=i_a, qa=q_a, ts=t_s, cs=c_s, qs=q_s, o0=mm_o0, co0=c_o0, o1=mm_o1, co1=c_o1,
-                     lpre=load_pre, lgo=load_go, lw=load_w, lx=load_x, lm=load_m, lp1=load_pre1)
+        table = dict(stt=stt, w=w, d=d, m=m, x=x_, qw=qw, qd=qd, qm=qm, qx=qx, m1=m1, ia=ia, qa=qa, s=s, qs=qs, o0=o0, o1a=o1a, o1=o1,
+                     lpre=load_pre, lgo=load_go, lw=load_w, lm=load_m, lx=load_x)
         with tc.manual_schedule():
             for token in PLAN.split():
                 part = token.split(".")
-                table[part[0]](*[int(a) if a not in ("s", "v") else a for a in part[1:]])
+                table[part[0]](*[int(v) if v not in ("s", "v") else v for v in part[1:]])

@@ -13,38 +13,24 @@ U8 = mybir.dt.uint8
 E4M3 = mybir.dt.float8_e4m3fn_x4
 E5M2 = mybir.dt.float8_e5m2_x4
 ALU = mybir.AluOpType
+
 P = 128
-NGRP = 3
-NWC = 2
-NDC = 2
-NDZ = 2
-NGA = 1
-NGS = 2
-NRES = 6
-NPRE = 4
-NGO = 2
-NWM = 3
-PLAN = (
-    "lw.0.0.2 lw.0.2.2 lpre.0.0.1 lgo.0.0.1 lpre.0.1.1 lgo.0.1.1 lpre.0.2.2 lgo.0.2.2 lw.1.0.2 lpre.1.0.2 lgo.1.0.2 lw.1.2.2 lpre.1.2.2 lgo.1.2.2 "
-    "lx.0 lx.1 lw.2.0.2 w.0.0.s w.0.1.v stt.0 stt.1 lpre.2.0.2 w.0.2.s w.0.3.v stt.2 stt.3 lgo.2.0.2 lw.2.2.2 "
-    "lpre.2.2.2 lgo.2.2.2 lw.3.0.2 lw.3.2.2 qw.0 d.0.0.s d.0.1.s d.0.2.v d.0.3.v w.1.0.s w.1.1.s qd.0 m1.0.0.s stt.4 "
-    "stt.5 lpre.3.0.2 stt.6 stt.7 lgo.3.0.2 lpre.3.2.2 lgo.3.2.2 m1.0.1.v d.1.0.s d.1.1.s w.1.2.s w.1.3.s lm.0.0.2 lm.0.2.2 "
-    "qw.1 m1.0.2.v d.1.2.s d.1.3.s m1.0.3.s x.0.0.s x.0.1.s qd.1 ia.0 x.1.0.s x.1.1.s stt.8 stt.9 m1.1.0.s "
-    "qx m1.1.1.s m1.1.2.s m1.1.3.s ia.1 w.2.0.s w.2.1.s s.0.0.0.s s.0.0.1.s w.2.2.s w.2.3.s lm.1.0.2 lm.1.2.2 s.0.1.0.s "
-    "s.0.1.1.s stt.10 stt.11 d.2.0.v d.2.1.s d.2.2.s d.2.3.s qa.0.0 qw.2 qd.2 o0.0.0.0.s o0.0.0.1.s w.3.0.s w.3.1.s "
-    "o0.0.0.2.s o0.0.0.3.s qs.0.0 stt.12 stt.13 stt.14 stt.15 m1.2.0.s qa.0.1 m1.2.1.s m1.2.2.s m1.2.3.v w.3.2.s w.3.3.s "
-    "d.3.0.s d.3.1.s qw.3 d.3.2.s d.3.3.s qd.3 ia.2 m.0.0.s m.0.1.s o0.0.1.0.s o0.0.1.1.s m.0.2.s m.0.3.v m1.3.0.s "
-    "m1.3.1.v m1.3.2.s m1.3.3.s qm.0 ia.3 m.1.0.s m.1.1.s o0.0.1.2.s o0.0.1.3.s m.1.2.s m.1.3.s qa.1.0 qa.1.1 qs.0.1 "
-    "o0.1.0.0.v o0.1.0.1.s s.1.0.0.s s.1.0.1.v o0.1.0.2.s o0.1.0.3.v o0.1.1.0.s o0.1.1.1.s qs.1.0 qm.1 s.1.1.0.v s.1.1.1.v o0.1.1.2.s o0.1.1.3.s "
-    "o1a.0.0 o1a.0.1 qs.1.1 o1.0.0.s o1.0.1.s o1a.0.2 o1a.0.3 o1.0.2.v o1.0.3.s o1a.1.0 o1a.1.1 o1.1.0.s o1.1.1.v o1a.1.2 "
-    "o1a.1.3 o1.1.2.v o1.1.3.s "
-)
+N = 512
+PAIRS = E // 2
+
+BUFS = {
+    "pre": 4, "grad": 2, "weights": 3, "x": 1,
+    "dz2": 2, "grouped": 3, "x_grouped": 1,
+    "wi_codes": 2, "wi_scales": 2, "dz2_codes": 2, "dz2_scales": 2,
+    "dz1": 2, "dz1_by_m": 1, "dz1_by_slot": 2, "result": 6,
+}
 
 
 def tile_flaxpositionwisemoelayer_pa_v_kernel(tc, dispatch_mask, x, wi, pre, grad_out, out_0, out_1):
     nc = tc.nc
+
     mask_rows = dispatch_mask.rearrange("g (p t) e c -> g p t (e c)", t=4)
-    x_rows = x.rearrange("g (p t) m -> g p t m", t=4)
+    x_rows = x.rearrange("g (p t) m -> p g t m", t=4)
     wi_rows = wi.rearrange("e (p t) h -> e p t h", t=4)
     pre_rows = pre.rearrange("e g c h -> e (g c) h").rearrange("e (p j) h -> e p j h", j=4)
     grad_rows = grad_out.rearrange("e g c h -> e (g c) h").rearrange("e (p j) h -> e p j h", j=4)
@@ -58,41 +44,22 @@ def tile_flaxpositionwisemoelayer_pa_v_kernel(tc, dispatch_mask, x, wi, pre, gra
 
         ident = keep.tile([P, P], F32, name="ident")
         make_identity(nc, ident[:])
+
         x_codes = keep.tile([P, G * S], U32, align_bytes=64, name="x_codes")
         x_scales = keep.tile([P, G * S], U8, align_bytes=64, name="x_scales")
-        mask_codes = keep.tile([P, G, 2 * S], U32, align_bytes=64, name="mask_codes")
-        mask_scales = keep.tile([P, G, 2 * S], U8, align_bytes=64, name="mask_scales")
-        dm_codes = keep.tile([P, 2, G, 512], U32, align_bytes=64, name="dm_codes")
-        dm_scales = keep.tile([P, 2, G, 512], U8, align_bytes=64, name="dm_scales")
-        dk_codes = keep.tile([P, 2, G, 512], U32, align_bytes=64, name="dk_codes")
-        dk_scales = keep.tile([P, 2, G, 512], U8, align_bytes=64, name="dk_scales")
-        st = {}
+        mask_codes = keep.tile([P, G, PAIRS * S], U32, align_bytes=64, name="mask_codes")
+        mask_scales = keep.tile([P, G, PAIRS * S], U8, align_bytes=64, name="mask_scales")
+        dz1_m_codes = keep.tile([P, PAIRS, G, N], U32, align_bytes=64, name="dz1_m_codes")
+        dz1_m_scales = keep.tile([P, PAIRS, G, N], U8, align_bytes=64, name="dz1_m_scales")
+        dz1_k_codes = keep.tile([P, PAIRS, G, N], U32, align_bytes=64, name="dz1_k_codes")
+        dz1_k_scales = keep.tile([P, PAIRS, G, N], U8, align_bytes=64, name="dz1_k_scales")
 
-        def tile_of(key, shape, dtype, tag, bufs):
-            if key not in st:
-                st[key] = ring.tile(shape, dtype, tag=tag, bufs=bufs, align_bytes=64, name="t_" + tag)
-            return st[key]
+        tiles = {}
 
-        def load(key, src, dtype, tag, bufs, j, n):
-            t = tile_of(key, [P, 4, src.shape[-1]], dtype, tag, bufs)
-            nc.sync.dma_start(out=t[:, j : j + n, :], in_=src[:, j : j + n, :])
-
-        def load_pre(e, j, n):
-            h = j // 2
-            t = tile_of(("pre", e, h), [P, 2, H], F32, "pre", NPRE)
-            nc.sync.dma_start(out=t[:, j - 2 * h : j - 2 * h + n, :], in_=pre_rows[e, :, j : j + n, :])
-
-        def load_go(e, j, n):
-            load(("go", e), grad_rows[e], BF16, "go", NGO, j, n)
-
-        def load_w(e, j, n):
-            load(("w", e), wi_rows[e], BF16, "wm", NWM, j, n)
-
-        def load_m(g, j, n):
-            load(("m", g), mask_rows[g], BF16, "wm", NWM, j, n)
-
-        def load_x(g):
-            load(("x", g), x_rows[g], BF16, "x", 2, 0, 4)
+        def ring_tile(kind, key, shape, dtype):
+            if (kind, key) not in tiles:
+                tiles[kind, key] = ring.tile(shape, dtype, tag=kind, bufs=BUFS[kind], align_bytes=64, name=kind)
+            return tiles[kind, key]
 
         def copy(engine, out, in_):
             if engine == "s":
@@ -100,134 +67,312 @@ def tile_flaxpositionwisemoelayer_pa_v_kernel(tc, dispatch_mask, x, wi, pre, gra
             else:
                 nc.vector.tensor_copy(out=out, in_=in_)
 
-        def stt(n):
-            e, j = divmod(n, 4)
-            h, u = divmod(j, 2)
-            dz2 = tile_of(("dz2", e, h), [P, 2, 2, 512], BF16, "dz2", NDZ)
-            nc.vector.scalar_tensor_tensor(
-                out=dz2[:, u].rearrange("p j (k b) -> p j k b", b=2),
-                in0=st["pre", e, h][:].rearrange("p j (k u b) -> p u j k b", u=2, b=2)[:, u],
-                scalar=0.0,
-                in1=st["go", e][:, 2 * h : 2 * h + 2, :].rearrange("p j (k u b) -> p u j k b", u=2, b=2)[:, u],
-                op0=ALU.is_gt,
-                op1=ALU.mult,
-            )
 
-        def new_bank():
-            bank = psum.tile([P, 2, 2, P], F32, tag="turn", bufs=4, name="bank")
-            return bank
+        def load_pre(e, j, n):
+            half, first = divmod(j, 2)
+            t = ring_tile("pre", (e, half), [P, 2, H], F32)
+            nc.sync.dma_start(out=t[:, first : first + n, :], in_=pre_rows[e, :, j : j + n, :])
 
-        def turn(eng, srcs, grp, block):
-            bank = psum.tile([P, 2, 2, P], F32, tag="turn", bufs=4, name="bank")
+        def load_grad(e, j, n):
+            t = ring_tile("grad", e, [P, 4, H], BF16)
+            nc.sync.dma_start(out=t[:, j : j + n, :], in_=grad_rows[e, :, j : j + n, :])
+
+        def load_wi(e, j, n):
+            t = ring_tile("weights", ("wi", e), [P, 4, H], BF16)
+            nc.sync.dma_start(out=t[:, j : j + n, :], in_=wi_rows[e, :, j : j + n, :])
+
+        def load_mask(g):
+            t = ring_tile("weights", ("mask", g), [P, 4, E * C], BF16)
+            nc.sync.dma_start(out=t[:], in_=mask_rows[g])
+
+        def load_x():
+            t = ring_tile("x", 0, [P, G, 4, M], BF16)
+            nc.sync.dma_start(out=t[:], in_=x_rows)
+
+
+        def turn(engine, source, grouped, block):
+            bank = psum.tile([P, 2, 2, P], F32, tag="turned", name="bank")
             for i in range(2):
                 for u in range(2):
-                    nc.tensor.transpose(bank[:, i, u, :], srcs(i, u), ident[:])
-            dst = grp[:].bitcast(F32)[:, 512 * block : 512 * (block + 1)]
-            copy(eng, dst.rearrange("p (i r u) -> p i r u", i=2, u=2), bank[:].rearrange("p i u r -> p i r u"))
+                    nc.tensor.transpose(bank[:, i, u, :], source(i, u), ident[:])
+            words = grouped[:].bitcast(F32)[:, N * block : N * (block + 1)]
+            copy(engine, words.rearrange("p (i r u) -> p i r u", i=2, u=2), bank[:].rearrange("p i u r -> p i r u"))
 
-        def grouped(key):
-            return tile_of(key, [P, 4096], BF16, "grp", NGRP)
+        def turn_row(engine, row, grouped, block):
+            words = row.bitcast(F32)
+            turn(engine, lambda i, u: words[:, 256 * i + u : 256 * (i + 1) : 2], grouped, block)
 
-        def w(e, t, eng):
-            words = st["w", e][:, t, :].bitcast(F32)
-            turn(eng, lambda a, u: words[:, 256 * a + u : 256 * (a + 1) : 2], grouped(("gw", e)), t)
+        def turn_wi(e, half, engines):
+            for t in range(2):
+                row = 2 * half + t
+                grouped = ring_tile("grouped", ("wi", e), [P, 4096], BF16)
+                turn_row(engines[t], tiles["weights", ("wi", e)][:, row, :], grouped, row)
 
-        def m(g, t, eng):
-            words = st["m", g][:, t, :].bitcast(F32)
-            turn(eng, lambda a, u: words[:, 256 * a + u : 256 * (a + 1) : 2], grouped(("gm", g)), t)
+        def turn_mask(g, half, engines):
+            for t in range(2):
+                row = 2 * half + t
+                grouped = ring_tile("grouped", ("mask", g), [P, 4096], BF16)
+                turn_row(engines[t], tiles["weights", ("mask", g)][:, row, :], grouped, row)
 
-        def d(e, j, eng):
-            h, a = divmod(j, 2)
-            dz2 = st["dz2", e, h]
-            turn(eng, lambda jj, u: dz2[:, u, jj, 256 * a : 256 * (a + 1)].bitcast(F32), grouped(("gd", e)), 2 * a + h)
+        def turn_x(g, engines):
+            rows = tiles["x", 0]
+            for h in range(2):
+                grouped = ring_tile("x_grouped", 0, [P, 4096], BF16)
+                turn(engines[h], lambda i, u: rows[:, g, 2 * h + i, :].bitcast(F32)[:, u::2], grouped, 2 * g + h)
 
-        def quantize(grp, dt, codes, scales):
-            nc.vector.quantize_mx(out=codes.bitcast(dt), scales=scales, in_=grp)
-
-        def qw(e):
-            codes = tile_of(("wc", e), [P, 1024], U32, "wc", NWC)
-            scales = tile_of(("ws", e), [P, 1024], U8, "ws", NWC)
-            quantize(st["gw", e][:], E4M3, codes[:], scales[:])
-
-        def qd(e):
-            codes = tile_of(("dc", e), [P, 1024], U32, "dc", NDC)
-            scales = tile_of(("ds", e), [P, 1024], U8, "ds", NDC)
-            quantize(st["gd", e][:], E5M2, codes[:], scales[:])
-
-        def qm(g):
-            quantize(st["gm", g][:], E4M3, mask_codes[:, g, :], mask_scales[:, g, :])
-
-        def x_(g, h, eng):
-            rows = st["x", g]
-            turn(eng, lambda i, u: rows[:, 2 * h + i, :].bitcast(F32)[:, u::2], tile_of(("gx",), [P, 4096], BF16, "gx", 1), 2 * g + h)
-
-        def qx():
-            quantize(st["gx",][:], E4M3, x_codes[:], x_scales[:])
-
-        def m1(e, t, eng):
-            pair, i = divmod(e, 2)
-            acc = psum.tile([P, 512], F32, tag="acc", bufs=4, name="acc")
+        def turn_dz2(e, half, engines):
+            dz2 = tiles["dz2", (e, half)]
             for a in range(2):
-                wcols = slice(256 * t + 128 * a, 256 * t + 128 * (a + 1))
-                dcols = slice(512 * a, 512 * (a + 1))
-                nc.tensor.matmul_mx(
-                    out=acc[:], lhsT=st["wc", e][:, wcols].bitcast(E4M3), lhsT_scale=st["ws", e][:, wcols],
-                    rhs=st["dc", e][:, dcols].bitcast(E5M2), rhs_scale=st["ds", e][:, dcols],
-                    start=(a == 0), stop=(a == 1))
-            dz1 = tile_of(("dz1", pair), [P, 4, G, 2, 256], BF16, "dz1", 2)
-            copy(eng, dz1[:, t, :, :, 128 * i : 128 * (i + 1)].rearrange("p g u (q b) -> p g u q b", b=2),
-                 acc[:].rearrange("p (u b g q) -> p g u q b", u=2, b=2, g=2))
+                grouped = ring_tile("grouped", ("dz2", e), [P, 4096], BF16)
+                turn(engines[a], lambda i, u: dz2[:, u, i, 256 * a : 256 * (a + 1)].bitcast(F32), grouped, 2 * a + half)
 
-        def ia(e):
+        def turn_dz1(pair, g, engines):
+            dz1 = tiles["dz1", pair]
+            for h in range(2):
+                grouped = ring_tile("dz1_by_slot", (pair, g), [P, 2048], BF16)
+                turn(engines[h], lambda i, u: dz1[:, 2 * h + i, g, u, :].bitcast(F32), grouped, h)
+
+
+        def relu_backward(e, half):
+            dz2 = ring_tile("dz2", (e, half), [P, 2, 2, N], BF16)
+            pre_words = tiles["pre", (e, half)][:].rearrange("p j (k u b) -> p u j k b", u=2, b=2)
+            grad = tiles["grad", e][:, 2 * half : 2 * half + 2, :].rearrange("p j (k u b) -> p u j k b", u=2, b=2)
+            for u in range(2):
+                nc.vector.scalar_tensor_tensor(
+                    out=dz2[:, u].rearrange("p j (k b) -> p j k b", b=2),
+                    in0=pre_words[:, u], scalar=0.0, in1=grad[:, u], op0=ALU.is_gt, op1=ALU.mult)
+
+        def quantize_wi(e):
+            codes = ring_tile("wi_codes", e, [P, 2 * M], U32)
+            scales = ring_tile("wi_scales", e, [P, 2 * M], U8)
+            nc.vector.quantize_mx(out=codes[:].bitcast(E4M3), scales=scales[:], in_=tiles["grouped", ("wi", e)][:])
+
+        def quantize_dz2(e, a):
+            codes = ring_tile("dz2_codes", e, [P, 2 * N], U32)
+            scales = ring_tile("dz2_scales", e, [P, 2 * N], U8)
+            cols = slice(N * a, N * (a + 1))
+            nc.vector.quantize_mx(
+                out=codes[:, cols].bitcast(E5M2), scales=scales[:, cols],
+                in_=tiles["grouped", ("dz2", e)][:, 4 * N * a : 4 * N * (a + 1)])
+
+        def quantize_mask(g):
+            nc.vector.quantize_mx(
+                out=mask_codes[:, g, :].bitcast(E4M3), scales=mask_scales[:, g, :], in_=tiles["grouped", ("mask", g)][:])
+
+        def quantize_x():
+            nc.vector.quantize_mx(out=x_codes[:].bitcast(E4M3), scales=x_scales[:], in_=tiles["x_grouped", 0][:])
+
+        def quantize_dz1_m(pair, g):
+            by_m = tiles["dz1_by_m", pair][:, g].rearrange("p i u s t -> p (i u s t)")
+            nc.vector.quantize_mx(
+                out=dz1_m_codes[:, pair, g, :].bitcast(E5M2), scales=dz1_m_scales[:, pair, g, :], in_=by_m)
+
+        def quantize_dz1_slots(pair, g):
+            nc.vector.quantize_mx(
+                out=dz1_k_codes[:, pair, g, :].bitcast(E5M2), scales=dz1_k_scales[:, pair, g, :],
+                in_=tiles["dz1_by_slot", (pair, g)][:])
+
+
+        def dh_pass(e, t, a):
+            if a == 0:
+                tiles["dh", (e, t)] = psum.tile([P, N], F32, tag="sums", name="dh")
+            w_cols = slice(256 * t + P * a, 256 * t + P * (a + 1))
+            d_cols = slice(N * a, N * (a + 1))
+            nc.tensor.matmul_mx(
+                out=tiles["dh", (e, t)][:],
+                lhsT=tiles["wi_codes", e][:, w_cols].bitcast(E4M3), lhsT_scale=tiles["wi_scales", e][:, w_cols],
+                rhs=tiles["dz2_codes", e][:, d_cols].bitcast(E5M2), rhs_scale=tiles["dz2_scales", e][:, d_cols],
+                start=(a == 0), stop=(a == 1))
+
+        def dh_first(e, t):
+            dh_pass(e, t, 0)
+
+        def dh_second(e, t, engine):
+            dh_pass(e, t, 1)
             pair, i = divmod(e, 2)
-            ga = tile_of(("ga", pair), [P, G, 2, 2, 128, 4], BF16, "ga", NGA)
-            nc.vector.tensor_copy(out=ga[:, :, i], in_=st["dz1", pair][:, :, :, :, 128 * i : 128 * (i + 1)].rearrange("p t g u s -> p g u s t"))
+            dz1 = ring_tile("dz1", pair, [P, 4, G, 2, 256], BF16)
+            copy(engine,
+                 dz1[:, t, :, :, P * i : P * (i + 1)].rearrange("p g u (q b) -> p g u q b", b=2),
+                 tiles["dh", (e, t)][:].rearrange("p (u b g q) -> p g u q b", u=2, b=2, g=2))
 
-        def qa(pair, g):
-            quantize(st["ga", pair][:, g].rearrange("p i u s t -> p (i u s t)"), E5M2, dm_codes[:, pair, g, :], dm_scales[:, pair, g, :])
+        def interleave_dz1(e):
+            pair, i = divmod(e, 2)
+            by_m = ring_tile("dz1_by_m", pair, [P, G, 2, 2, P, 4], BF16)
+            nc.vector.tensor_copy(
+                out=by_m[:, :, i], in_=tiles["dz1", pair][:, :, :, :, P * i : P * (i + 1)].rearrange("p t g u s -> p g u s t"))
 
-        def s(pair, g, h, eng):
-            dz1 = st["dz1", pair]
-            turn(eng, lambda i, u: dz1[:, 2 * h + i, g, u, :].bitcast(F32), tile_of(("gs", pair, g), [P, 2048], BF16, "gs", NGS), h)
 
-        def qs(pair, g):
-            quantize(st["gs", pair, g][:], E5M2, dk_codes[:, pair, g, :], dk_scales[:, pair, g, :])
+        def output_0(pair, g, half, engines):
+            result = ring_tile("result", ("out_0", pair, g, half), [P, 2, N], F32)
+            for t in range(2):
+                acc = psum.tile([P, N], F32, tag="sums", name="acc")
+                cols = slice(S * g + P * (2 * half + t), S * g + P * (2 * half + t + 1))
+                nc.tensor.matmul_mx(
+                    out=acc[:], lhsT=x_codes[:, cols].bitcast(E4M3), lhsT_scale=x_scales[:, cols],
+                    rhs=dz1_m_codes[:, pair, g, :].bitcast(E5M2), rhs_scale=dz1_m_scales[:, pair, g, :],
+                    start=True, stop=True)
+                copy(engines[t],
+                     result[:, t, :].rearrange("p (i q u b) -> p i q u b", i=2, u=2, b=2),
+                     acc[:].rearrange("p (i u q b) -> p i q u b", i=2, u=2, b=2))
+            nc.sync.dma_start(out=out0_rows[g, :, 2 * half : 2 * half + 2, N * pair : N * (pair + 1)], in_=result[:])
 
-        def o0(pair, g, t, eng):
-            acc = psum.tile([P, 512], F32, tag="acc", bufs=4, name="acc")
-            cols = slice(512 * g + 128 * t, 512 * g + 128 * (t + 1))
-            nc.tensor.matmul_mx(
-                out=acc[:], lhsT=x_codes[:, cols].bitcast(E4M3), lhsT_scale=x_scales[:, cols],
-                rhs=dm_codes[:, pair, g, :].bitcast(E5M2), rhs_scale=dm_scales[:, pair, g, :], start=True, stop=True)
-            res = tile_of(("r0", pair, g, t // 2), [P, 2, 512], F32, "res", NRES)
-            copy(eng, res[:, t % 2, :].rearrange("p (i q u b) -> p i q u b", i=2, u=2, b=2),
-                 acc[:].rearrange("p (i u q b) -> p i q u b", i=2, u=2, b=2))
-            if t % 2 == 1:
-                nc.sync.dma_start(out=out0_rows[g, :, t - 1 : t + 1, 512 * pair : 512 * (pair + 1)], in_=res[:])
-
-        def o1_pass(g, t, pair):
+        def out1_pass(g, row, pair):
             if pair == 0:
-                tag = "acc" if g == 0 else "turn"
-                st["o1", g, t] = psum.tile([P, 512], F32, tag=tag, bufs=4, name="acc1")
-            cols = slice(256 * t + 128 * pair, 256 * t + 128 * (pair + 1))
+                tiles["out_1", (g, row)] = psum.tile([P, N], F32, tag="sums" if g == 0 else "turned", name="acc1")
+            cols = slice(256 * row + P * pair, 256 * row + P * (pair + 1))
             nc.tensor.matmul_mx(
-                out=st["o1", g, t][:], lhsT=mask_codes[:, g, cols].bitcast(E4M3), lhsT_scale=mask_scales[:, g, cols],
-                rhs=dk_codes[:, pair, g, :].bitcast(E5M2), rhs_scale=dk_scales[:, pair, g, :],
+                out=tiles["out_1", (g, row)][:],
+                lhsT=mask_codes[:, g, cols].bitcast(E4M3), lhsT_scale=mask_scales[:, g, cols],
+                rhs=dz1_k_codes[:, pair, g, :].bitcast(E5M2), rhs_scale=dz1_k_scales[:, pair, g, :],
                 start=(pair == 0), stop=(pair == 1))
 
-        def o1a(g, t):
-            o1_pass(g, t, 0)
+        def output_1_first(g, half):
+            for t in range(2):
+                out1_pass(g, 2 * half + t, 0)
 
-        def o1(g, t, eng):
-            o1_pass(g, t, 1)
-            res = tile_of(("r1", g, t // 2), [P, 2, 512], F32, "res", NRES)
-            copy(eng, res[:, t % 2, :].rearrange("p (m t) -> p m t", t=4), st["o1", g, t][:].rearrange("p (t m) -> p m t", t=4))
-            if t % 2 == 1:
-                nc.sync.dma_start(out=out1_rows[g, :, t - 1 : t + 1, :], in_=res[:])
+        def output_1_second(g, half, engines):
+            result = ring_tile("result", ("out_1", g, half), [P, 2, N], F32)
+            for t in range(2):
+                row = 2 * half + t
+                out1_pass(g, row, 1)
+                copy(engines[t],
+                     result[:, t, :].rearrange("p (m t) -> p m t", t=4),
+                     tiles["out_1", (g, row)][:].rearrange("p (t m) -> p m t", t=4))
+                if (g, half) == (G - 1, 1):
+                    nc.sync.dma_start(out=out1_rows[g, :, row, :], in_=result[:, t, :])
+            if (g, half) != (G - 1, 1):
+                nc.sync.dma_start(out=out1_rows[g, :, 2 * half : 2 * half + 2, :], in_=result[:])
 
-        table = dict(stt=stt, w=w, d=d, m=m, x=x_, qw=qw, qd=qd, qm=qm, qx=qx, m1=m1, ia=ia, qa=qa, s=s, qs=qs, o0=o0, o1a=o1a, o1=o1,
-                     lpre=load_pre, lgo=load_go, lw=load_w, lm=load_m, lx=load_x)
         with tc.manual_schedule():
-            for token in PLAN.split():
-                part = token.split(".")
-                table[part[0]](*[int(v) if v not in ("s", "v") else v for v in part[1:]])
+            load_wi(0, 0, 2)
+            load_pre(0, 0, 1)
+            load_grad(0, 0, 1)
+            load_pre(0, 1, 1)
+            load_grad(0, 1, 1)
+            load_pre(0, 2, 2)
+            load_grad(0, 2, 2)
+            load_wi(0, 2, 2)
+            load_grad(1, 0, 4)
+            load_wi(1, 0, 4)
+            load_pre(1, 0, 2)
+            load_pre(1, 2, 2)
+            load_x()
+            turn_wi(0, 0, "ss")
+            relu_backward(0, 0)
+            relu_backward(0, 1)
+            load_grad(2, 0, 4)
+            load_pre(2, 0, 2)
+            load_wi(2, 0, 4)
+            load_pre(2, 2, 2)
+            turn_wi(0, 1, "sv")
+            load_wi(3, 0, 4)
+            turn_dz2(0, 0, "vv")
+            quantize_wi(0)
+            turn_dz2(0, 1, "ss")
+            quantize_dz2(0, 0)
+            turn_wi(1, 0, "ss")
+            dh_first(0, 0)
+            dh_first(0, 1)
+            quantize_dz2(0, 1)
+            dh_second(0, 0, "s")
+            dh_first(0, 2)
+            relu_backward(1, 0)
+            load_pre(3, 0, 2)
+            dh_second(0, 1, "s")
+            relu_backward(1, 1)
+            load_grad(3, 0, 4)
+            load_pre(3, 2, 2)
+            dh_first(0, 3)
+            dh_second(0, 2, "s")
+            turn_wi(1, 1, "ss")
+            load_mask(0)
+            quantize_wi(1)
+            dh_second(0, 3, "s")
+            turn_dz2(1, 0, "ss")
+            turn_dz2(1, 1, "ss")
+            turn_x(0, "ss")
+            turn_x(1, "ss")
+            quantize_dz2(1, 0)
+            dh_first(1, 0)
+            dh_first(1, 1)
+            quantize_dz2(1, 1)
+            interleave_dz1(0)
+            dh_second(1, 0, "s")
+            dh_second(1, 1, "v")
+            dh_first(1, 2)
+            dh_first(1, 3)
+            relu_backward(2, 0)
+            dh_second(1, 2, "s")
+            dh_second(1, 3, "s")
+            turn_dz1(0, 0, "ss")
+            interleave_dz1(1)
+            quantize_dz1_m(0, 0)
+            quantize_dz1_m(0, 1)
+            relu_backward(2, 1)
+            turn_wi(2, 0, "ss")
+            turn_dz2(2, 0, "ss")
+            quantize_x()
+            turn_dz1(0, 1, "ss")
+            turn_wi(2, 1, "ss")
+            load_mask(1)
+            turn_wi(3, 0, "ss")
+            turn_dz2(2, 1, "ss")
+            quantize_wi(2)
+            turn_wi(3, 1, "ss")
+            quantize_dz2(2, 0)
+            output_0(0, 0, 0, "ss")
+            dh_first(2, 0)
+            dh_first(2, 1)
+            quantize_dz2(2, 1)
+            dh_second(2, 0, "s")
+            dh_first(2, 2)
+            relu_backward(3, 0)
+            relu_backward(3, 1)
+            dh_second(2, 1, "s")
+            dh_second(2, 2, "s")
+            output_0(0, 0, 1, "ss")
+            dh_first(2, 3)
+            dh_second(2, 3, "s")
+            turn_dz2(3, 0, "vs")
+            turn_dz2(3, 1, "ss")
+            quantize_wi(3)
+            quantize_dz2(3, 0)
+            quantize_dz2(3, 1)
+            turn_mask(0, 0, "ss")
+            turn_mask(0, 1, "ss")
+            interleave_dz1(2)
+            quantize_dz1_slots(0, 0)
+            dh_first(3, 0)
+            dh_first(3, 1)
+            dh_first(3, 2)
+            dh_second(3, 0, "s")
+            dh_first(3, 3)
+            dh_second(3, 1, "v")
+            dh_second(3, 2, "s")
+            dh_second(3, 3, "v")
+            output_0(0, 1, 0, "ss")
+            output_0(0, 1, 1, "ss")
+            turn_mask(1, 0, "ss")
+            interleave_dz1(3)
+            quantize_dz1_m(1, 0)
+            turn_dz1(1, 0, "vv")
+            output_0(1, 0, 0, "sv")
+            output_0(1, 0, 1, "ss")
+            quantize_dz1_m(1, 1)
+            quantize_mask(0)
+            turn_mask(1, 1, "sv")
+            quantize_dz1_slots(0, 1)
+            output_0(1, 1, 0, "ss")
+            output_0(1, 1, 1, "ss")
+            quantize_dz1_slots(1, 0)
+            quantize_mask(1)
+            turn_dz1(1, 1, "ss")
+            output_1_first(0, 0)
+            output_1_second(0, 0, "sv")
+            output_1_first(0, 1)
+            quantize_dz1_slots(1, 1)
+            output_1_second(0, 1, "sv")
+            output_1_first(1, 0)
+            output_1_second(1, 0, "sv")
+            output_1_first(1, 1)
+            output_1_second(1, 1, "sv")

from contextlib import ExitStack

import concourse.mybir as mybir
from concourse.masks import make_identity

G, S, M, H, E, C = 2, 512, 512, 1024, 4, 256
FLOPS = 2 * E * G * C * H * M + 2 * 2 * G * S * M * E * C

F32 = mybir.dt.float32
BF16 = mybir.dt.bfloat16
U32 = mybir.dt.uint32
U8 = mybir.dt.uint8
E4M3 = mybir.dt.float8_e4m3fn_x4
E5M2 = mybir.dt.float8_e5m2_x4
ALU = mybir.AluOpType

P = 128
N = 512
PAIRS = E // 2

BUFS = {
    "pre": 4, "grad": 2, "weights": 3, "x": 1,
    "dz2": 2, "grouped": 3, "x_grouped": 1,
    "wi_codes": 2, "wi_scales": 2, "dz2_codes": 2, "dz2_scales": 2,
    "dz1": 2, "dz1_by_m": 1, "dz1_by_slot": 2, "result": 6,
}


def tile_flaxpositionwisemoelayer_pa_v_kernel(tc, dispatch_mask, x, wi, pre, grad_out, out_0, out_1):
    nc = tc.nc

    mask_rows = dispatch_mask.rearrange("g (p t) e c -> g p t (e c)", t=4)
    x_rows = x.rearrange("g (p t) m -> p g t m", t=4)
    wi_rows = wi.rearrange("e (p t) h -> e p t h", t=4)
    pre_rows = pre.rearrange("e g c h -> e (g c) h").rearrange("e (p j) h -> e p j h", j=4)
    grad_rows = grad_out.rearrange("e g c h -> e (g c) h").rearrange("e (p j) h -> e p j h", j=4)
    out0_rows = out_0.rearrange("g (p t) e c -> g p t (e c)", t=4)
    out1_rows = out_1.rearrange("g (p t) m -> g p t m", t=4)

    with ExitStack() as ctx:
        keep = ctx.enter_context(tc.tile_pool(name="keep", bufs=1))
        ring = ctx.enter_context(tc.tile_pool(name="ring", bufs=1))
        psum = ctx.enter_context(tc.psum_pool(name="psum", bufs=4))

        ident = keep.tile([P, P], F32, name="ident")
        make_identity(nc, ident[:])

        x_codes = keep.tile([P, G * S], U32, align_bytes=64, name="x_codes")
        x_scales = keep.tile([P, G * S], U8, align_bytes=64, name="x_scales")
        mask_codes = keep.tile([P, G, PAIRS * S], U32, align_bytes=64, name="mask_codes")
        mask_scales = keep.tile([P, G, PAIRS * S], U8, align_bytes=64, name="mask_scales")
        dz1_m_codes = keep.tile([P, PAIRS, G, N], U32, align_bytes=64, name="dz1_m_codes")
        dz1_m_scales = keep.tile([P, PAIRS, G, N], U8, align_bytes=64, name="dz1_m_scales")
        dz1_k_codes = keep.tile([P, PAIRS, G, N], U32, align_bytes=64, name="dz1_k_codes")
        dz1_k_scales = keep.tile([P, PAIRS, G, N], U8, align_bytes=64, name="dz1_k_scales")

        tiles = {}

        def ring_tile(kind, key, shape, dtype):
            if (kind, key) not in tiles:
                tiles[kind, key] = ring.tile(shape, dtype, tag=kind, bufs=BUFS[kind], align_bytes=64, name=kind)
            return tiles[kind, key]

        def copy(engine, out, in_):
            if engine == "s":
                nc.scalar.copy(out=out, in_=in_)
            else:
                nc.vector.tensor_copy(out=out, in_=in_)


        def load_pre(e, j, n):
            half, first = divmod(j, 2)
            t = ring_tile("pre", (e, half), [P, 2, H], F32)
            nc.sync.dma_start(out=t[:, first : first + n, :], in_=pre_rows[e, :, j : j + n, :])

        def load_grad(e, j, n):
            t = ring_tile("grad", e, [P, 4, H], BF16)
            nc.sync.dma_start(out=t[:, j : j + n, :], in_=grad_rows[e, :, j : j + n, :])

        def load_wi(e, j, n):
            t = ring_tile("weights", ("wi", e), [P, 4, H], BF16)
            nc.sync.dma_start(out=t[:, j : j + n, :], in_=wi_rows[e, :, j : j + n, :])

        def load_mask(g):
            t = ring_tile("weights", ("mask", g), [P, 4, E * C], BF16)
            nc.sync.dma_start(out=t[:], in_=mask_rows[g])

        def load_x():
            t = ring_tile("x", 0, [P, G, 4, M], BF16)
            nc.sync.dma_start(out=t[:], in_=x_rows)


        def turn(engine, source, grouped, block):
            bank = psum.tile([P, 2, 2, P], F32, tag="turned", name="bank")
            for i in range(2):
                for u in range(2):
                    nc.tensor.transpose(bank[:, i, u, :], source(i, u), ident[:])
            words = grouped[:].bitcast(F32)[:, N * block : N * (block + 1)]
            copy(engine, words.rearrange("p (i r u) -> p i r u", i=2, u=2), bank[:].rearrange("p i u r -> p i r u"))

        def turn_row(engine, row, grouped, block):
            words = row.bitcast(F32)
            turn(engine, lambda i, u: words[:, 256 * i + u : 256 * (i + 1) : 2], grouped, block)

        def turn_wi(e, half, engines):
            for t in range(2):
                row = 2 * half + t
                grouped = ring_tile("grouped", ("wi", e), [P, 4096], BF16)
                turn_row(engines[t], tiles["weights", ("wi", e)][:, row, :], grouped, row)

        def turn_mask(g, half, engines):
            for t in range(2):
                row = 2 * half + t
                grouped = ring_tile("grouped", ("mask", g), [P, 4096], BF16)
                turn_row(engines[t], tiles["weights", ("mask", g)][:, row, :], grouped, row)

        def turn_x(g, engines):
            rows = tiles["x", 0]
            for h in range(2):
                grouped = ring_tile("x_grouped", 0, [P, 4096], BF16)
                turn(engines[h], lambda i, u: rows[:, g, 2 * h + i, :].bitcast(F32)[:, u::2], grouped, 2 * g + h)

        def turn_dz2(e, half, engines):
            dz2 = tiles["dz2", (e, half)]
            for a in range(2):
                grouped = ring_tile("grouped", ("dz2", e), [P, 4096], BF16)
                turn(engines[a], lambda i, u: dz2[:, u, i, 256 * a : 256 * (a + 1)].bitcast(F32), grouped, 2 * a + half)

        def turn_dz1(pair, g, engines):
            dz1 = tiles["dz1", pair]
            for h in range(2):
                grouped = ring_tile("dz1_by_slot", (pair, g), [P, 2048], BF16)
                turn(engines[h], lambda i, u: dz1[:, 2 * h + i, g, u, :].bitcast(F32), grouped, h)


        def relu_backward(e, half):
            dz2 = ring_tile("dz2", (e, half), [P, 2, 2, N], BF16)
            pre_words = tiles["pre", (e, half)][:].rearrange("p j (k u b) -> p u j k b", u=2, b=2)
            grad = tiles["grad", e][:, 2 * half : 2 * half + 2, :].rearrange("p j (k u b) -> p u j k b", u=2, b=2)
            for u in range(2):
                nc.vector.scalar_tensor_tensor(
                    out=dz2[:, u].rearrange("p j (k b) -> p j k b", b=2),
                    in0=pre_words[:, u], scalar=0.0, in1=grad[:, u], op0=ALU.is_gt, op1=ALU.mult)

        def quantize_wi(e):
            codes = ring_tile("wi_codes", e, [P, 2 * M], U32)
            scales = ring_tile("wi_scales", e, [P, 2 * M], U8)
            nc.vector.quantize_mx(out=codes[:].bitcast(E4M3), scales=scales[:], in_=tiles["grouped", ("wi", e)][:])

        def quantize_dz2(e, a):
            codes = ring_tile("dz2_codes", e, [P, 2 * N], U32)
            scales = ring_tile("dz2_scales", e, [P, 2 * N], U8)
            cols = slice(N * a, N * (a + 1))
            nc.vector.quantize_mx(
                out=codes[:, cols].bitcast(E5M2), scales=scales[:, cols],
                in_=tiles["grouped", ("dz2", e)][:, 4 * N * a : 4 * N * (a + 1)])

        def quantize_mask(g):
            nc.vector.quantize_mx(
                out=mask_codes[:, g, :].bitcast(E4M3), scales=mask_scales[:, g, :], in_=tiles["grouped", ("mask", g)][:])

        def quantize_x():
            nc.vector.quantize_mx(out=x_codes[:].bitcast(E4M3), scales=x_scales[:], in_=tiles["x_grouped", 0][:])

        def quantize_dz1_m(pair, g):
            by_m = tiles["dz1_by_m", pair][:, g].rearrange("p i u s t -> p (i u s t)")
            nc.vector.quantize_mx(
                out=dz1_m_codes[:, pair, g, :].bitcast(E5M2), scales=dz1_m_scales[:, pair, g, :], in_=by_m)

        def quantize_dz1_slots(pair, g):
            nc.vector.quantize_mx(
                out=dz1_k_codes[:, pair, g, :].bitcast(E5M2), scales=dz1_k_scales[:, pair, g, :],
                in_=tiles["dz1_by_slot", (pair, g)][:])


        def dh_pass(e, t, a):
            if a == 0:
                tiles["dh", (e, t)] = psum.tile([P, N], F32, tag="sums", name="dh")
            w_cols = slice(256 * t + P * a, 256 * t + P * (a + 1))
            d_cols = slice(N * a, N * (a + 1))
            nc.tensor.matmul_mx(
                out=tiles["dh", (e, t)][:],
                lhsT=tiles["wi_codes", e][:, w_cols].bitcast(E4M3), lhsT_scale=tiles["wi_scales", e][:, w_cols],
                rhs=tiles["dz2_codes", e][:, d_cols].bitcast(E5M2), rhs_scale=tiles["dz2_scales", e][:, d_cols],
                start=(a == 0), stop=(a == 1))

        def dh_first(e, t):
            dh_pass(e, t, 0)

        def dh_second(e, t, engine):
            dh_pass(e, t, 1)
            pair, i = divmod(e, 2)
            dz1 = ring_tile("dz1", pair, [P, 4, G, 2, 256], BF16)
            copy(engine,
                 dz1[:, t, :, :, P * i : P * (i + 1)].rearrange("p g u (q b) -> p g u q b", b=2),
                 tiles["dh", (e, t)][:].rearrange("p (u b g q) -> p g u q b", u=2, b=2, g=2))

        def interleave_dz1(e):
            pair, i = divmod(e, 2)
            by_m = ring_tile("dz1_by_m", pair, [P, G, 2, 2, P, 4], BF16)
            nc.vector.tensor_copy(
                out=by_m[:, :, i], in_=tiles["dz1", pair][:, :, :, :, P * i : P * (i + 1)].rearrange("p t g u s -> p g u s t"))


        def output_0(pair, g, half, engines):
            result = ring_tile("result", ("out_0", pair, g, half), [P, 2, N], F32)
            for t in range(2):
                acc = psum.tile([P, N], F32, tag="sums", name="acc")
                cols = slice(S * g + P * (2 * half + t), S * g + P * (2 * half + t + 1))
                nc.tensor.matmul_mx(
                    out=acc[:], lhsT=x_codes[:, cols].bitcast(E4M3), lhsT_scale=x_scales[:, cols],
                    rhs=dz1_m_codes[:, pair, g, :].bitcast(E5M2), rhs_scale=dz1_m_scales[:, pair, g, :],
                    start=True, stop=True)
                copy(engines[t],
                     result[:, t, :].rearrange("p (i q u b) -> p i q u b", i=2, u=2, b=2),
                     acc[:].rearrange("p (i u q b) -> p i q u b", i=2, u=2, b=2))
            nc.sync.dma_start(out=out0_rows[g, :, 2 * half : 2 * half + 2, N * pair : N * (pair + 1)], in_=result[:])

        def out1_pass(g, row, pair):
            if pair == 0:
                tiles["out_1", (g, row)] = psum.tile([P, N], F32, tag="sums" if g == 0 else "turned", name="acc1")
            cols = slice(256 * row + P * pair, 256 * row + P * (pair + 1))
            nc.tensor.matmul_mx(
                out=tiles["out_1", (g, row)][:],
                lhsT=mask_codes[:, g, cols].bitcast(E4M3), lhsT_scale=mask_scales[:, g, cols],
                rhs=dz1_k_codes[:, pair, g, :].bitcast(E5M2), rhs_scale=dz1_k_scales[:, pair, g, :],
                start=(pair == 0), stop=(pair == 1))

        def output_1_first(g, half):
            for t in range(2):
                out1_pass(g, 2 * half + t, 0)

        def output_1_second(g, half, engines):
            result = ring_tile("result", ("out_1", g, half), [P, 2, N], F32)
            for t in range(2):
                row = 2 * half + t
                out1_pass(g, row, 1)
                copy(engines[t],
                     result[:, t, :].rearrange("p (m t) -> p m t", t=4),
                     tiles["out_1", (g, row)][:].rearrange("p (t m) -> p m t", t=4))
                if (g, half) == (G - 1, 1):
                    nc.sync.dma_start(out=out1_rows[g, :, row, :], in_=result[:, t, :])
            if (g, half) != (G - 1, 1):
                nc.sync.dma_start(out=out1_rows[g, :, 2 * half : 2 * half + 2, :], in_=result[:])

        with tc.manual_schedule():
            load_wi(0, 0, 2)
            load_pre(0, 0, 1)
            load_grad(0, 0, 1)
            load_pre(0, 1, 1)
            load_grad(0, 1, 1)
            load_pre(0, 2, 2)
            load_grad(0, 2, 2)
            load_wi(0, 2, 2)
            load_grad(1, 0, 4)
            load_wi(1, 0, 4)
            load_pre(1, 0, 2)
            load_pre(1, 2, 2)
            load_x()
            turn_wi(0, 0, "ss")
            relu_backward(0, 0)
            relu_backward(0, 1)
            load_grad(2, 0, 4)
            load_pre(2, 0, 2)
            load_wi(2, 0, 4)
            load_pre(2, 2, 2)
            turn_wi(0, 1, "sv")
            load_wi(3, 0, 4)
            turn_dz2(0, 0, "vv")
            quantize_wi(0)
            turn_dz2(0, 1, "ss")
            quantize_dz2(0, 0)
            turn_wi(1, 0, "ss")
            dh_first(0, 0)
            dh_first(0, 1)
            quantize_dz2(0, 1)
            dh_second(0, 0, "s")
            dh_first(0, 2)
            relu_backward(1, 0)
            load_pre(3, 0, 2)
            dh_second(0, 1, "s")
            relu_backward(1, 1)
            load_grad(3, 0, 4)
            load_pre(3, 2, 2)
            dh_first(0, 3)
            dh_second(0, 2, "s")
            turn_wi(1, 1, "ss")
            load_mask(0)
            quantize_wi(1)
            dh_second(0, 3, "s")
            turn_dz2(1, 0, "ss")
            turn_dz2(1, 1, "ss")
            turn_x(0, "ss")
            turn_x(1, "ss")
            quantize_dz2(1, 0)
            dh_first(1, 0)
            dh_first(1, 1)
            quantize_dz2(1, 1)
            interleave_dz1(0)
            dh_second(1, 0, "s")
            dh_second(1, 1, "v")
            dh_first(1, 2)
            dh_first(1, 3)
            relu_backward(2, 0)
            dh_second(1, 2, "s")
            dh_second(1, 3, "s")
            turn_dz1(0, 0, "ss")
            interleave_dz1(1)
            quantize_dz1_m(0, 0)
            quantize_dz1_m(0, 1)
            relu_backward(2, 1)
            turn_wi(2, 0, "ss")
            turn_dz2(2, 0, "ss")
            quantize_x()
            turn_dz1(0, 1, "ss")
            turn_wi(2, 1, "ss")
            load_mask(1)
            turn_wi(3, 0, "ss")
            turn_dz2(2, 1, "ss")
            quantize_wi(2)
            turn_wi(3, 1, "ss")
            quantize_dz2(2, 0)
            output_0(0, 0, 0, "ss")
            dh_first(2, 0)
            dh_first(2, 1)
            quantize_dz2(2, 1)
            dh_second(2, 0, "s")
            dh_first(2, 2)
            relu_backward(3, 0)
            relu_backward(3, 1)
            dh_second(2, 1, "s")
            dh_second(2, 2, "s")
            output_0(0, 0, 1, "ss")
            dh_first(2, 3)
            dh_second(2, 3, "s")
            turn_dz2(3, 0, "vs")
            turn_dz2(3, 1, "ss")
            quantize_wi(3)
            quantize_dz2(3, 0)
            quantize_dz2(3, 1)
            turn_mask(0, 0, "ss")
            turn_mask(0, 1, "ss")
            interleave_dz1(2)
            quantize_dz1_slots(0, 0)
            dh_first(3, 0)
            dh_first(3, 1)
            dh_first(3, 2)
            dh_second(3, 0, "s")
            dh_first(3, 3)
            dh_second(3, 1, "v")
            dh_second(3, 2, "s")
            dh_second(3, 3, "v")
            output_0(0, 1, 0, "ss")
            output_0(0, 1, 1, "ss")
            turn_mask(1, 0, "ss")
            interleave_dz1(3)
            quantize_dz1_m(1, 0)
            turn_dz1(1, 0, "vv")
            output_0(1, 0, 0, "sv")
            output_0(1, 0, 1, "ss")
            quantize_dz1_m(1, 1)
            quantize_mask(0)
            turn_mask(1, 1, "sv")
            quantize_dz1_slots(0, 1)
            output_0(1, 1, 0, "ss")
            output_0(1, 1, 1, "ss")
            quantize_dz1_slots(1, 0)
            quantize_mask(1)
            turn_dz1(1, 1, "ss")
            output_1_first(0, 0)
            output_1_second(0, 0, "sv")
            output_1_first(0, 1)
            quantize_dz1_slots(1, 1)
            output_1_second(0, 1, "sv")
            output_1_first(1, 0)
            output_1_second(1, 0, "sv")
            output_1_first(1, 1)
            output_1_second(1, 1, "sv")
